import numpy as np
import ml_dtypes


def mxq(x, axis, fmt="e4m3"):
    dtype, down = {"e4m3": (ml_dtypes.float8_e4m3fn, 7), "e5m2": (ml_dtypes.float8_e5m2, 14)}[fmt]
    v = np.moveaxis(np.asarray(x, np.float32).astype(ml_dtypes.bfloat16).astype(np.float64), axis, -1)
    blocks = v.reshape(v.shape[:-1] + (-1, 32))
    amax = np.abs(blocks).max(-1, keepdims=True)
    byte = np.maximum(np.where(amax > 0, np.frexp(amax)[1] - 1 + 127, 0) - down, 1)
    scale = np.exp2(byte - 127.0)
    codes = (blocks / scale).astype(np.float32).astype(dtype).astype(np.float64)
    return np.moveaxis((codes * scale).reshape(v.shape), -1, axis)


WIDE = False


def mx_kscale(k):
    if not WIDE:
        return np.ones(k)
    levels = np.array([10, -10, 5, -5, 0])
    if k % 512:
        return np.exp2(np.random.permutation(np.resize(levels, k // 32))).repeat(32)
    a = np.empty((k // 512, 16))
    for p in range(k // 512):
        a[p, :8] = np.random.permutation(np.resize(levels, 8))
        for g in range(8):
            far = levels[np.abs(levels - a[p, g]) >= 10]
            a[p, g + 8] = far[np.random.randint(len(far))]
    return np.exp2(a.ravel()).repeat(32)


BF16 = ml_dtypes.bfloat16


def bf(x):
    return np.asarray(x, np.float32).astype(BF16)


def f64(x):
    return np.asarray(x).astype(np.float64)


B, SI, ST, DM, H, D = 1, 768, 256, 1024, 8, 128
S = ST + SI
HD = H * D
EPS = 1e-6


def rms_norm(x, gamma):
    var = np.mean(x * x, axis=-1, keepdims=True)
    return x * (1.0 / np.sqrt(var + EPS)) * gamma


def apply_rotary(x, cos, sin):
    xr = x.reshape(B, S, H, D // 2, 2)
    x1, x2 = xr[..., 0], xr[..., 1]
    rot = np.stack([-x2, x1], axis=-1).reshape(B, S, H, D)
    return x * cos[None, :, None, :] + rot * sin[None, :, None, :]


def heads(y):
    return y.reshape(B, -1, H, D)


def setup_inputs():
    s = mx_kscale(DM)
    w = 1.0 / np.sqrt(DM)
    pos = np.arange(S)[:, None]
    inv = 1.0 / (10000.0 ** (np.arange(0, D, 2) / D))
    ang = np.repeat(pos * inv[None, :], 2, axis=-1)
    inp = {"hidden_states": bf(np.random.standard_normal((B, SI, DM)) * s),
           "encoder_hidden_states": bf(np.random.standard_normal((B, ST, DM)) * s),
           "rope_cos": bf(np.cos(ang)), "rope_sin": bf(np.sin(ang))}
    for n in ["Wq", "Wk", "Waq", "Wak"]:
        inp[n] = bf(np.random.standard_normal((DM, HD)) * w / s[:, None])
    for n in ["bq", "bk", "baq", "bak"]:
        inp[n] = bf(np.random.standard_normal(HD) * 0.3)
    for n in ["g_q", "g_k", "g_aq", "g_ak"]:
        inp[n] = bf(1.5 * (1.0 + 0.1 * np.random.standard_normal(D)))
    return inp


def reference(hidden_states, encoder_hidden_states, rope_cos, rope_sin, Wq, bq, Wk, bk, Waq, baq, Wak, bak, g_q, g_k, g_aq, g_ak):
    xq = mxq(f64(hidden_states), 2, "e4m3")
    cq = mxq(f64(encoder_hidden_states), 2, "e4m3")
    q = rms_norm(heads((xq @ mxq(f64(Wq), 0, "e4m3")) + f64(bq)), f64(g_q))
    k = rms_norm(heads((xq @ mxq(f64(Wk), 0, "e4m3")) + f64(bk)), f64(g_k))
    eq = rms_norm(heads((cq @ mxq(f64(Waq), 0, "e4m3")) + f64(baq)), f64(g_aq))
    ek = rms_norm(heads((cq @ mxq(f64(Wak), 0, "e4m3")) + f64(bak)), f64(g_ak))
    q = np.concatenate([eq, q], axis=1)
    k = np.concatenate([ek, k], axis=1)
    return apply_rotary(q, f64(rope_cos), f64(rope_sin)), apply_rotary(k, f64(rope_cos), f64(rope_sin))

@@ -1,0 +1,356 @@
+from contextlib import ExitStack
+
+import concourse.mybir as mybir
+from concourse.masks import make_identity
+
+F32 = mybir.dt.float32
+BF16 = mybir.dt.bfloat16
+U32 = mybir.dt.uint32
+U8 = mybir.dt.uint8
+I32 = mybir.dt.int32
+FP8X4 = mybir.dt.float8_e4m3fn_x4
+ALU = mybir.AluOpType
+ACT = mybir.ActivationFunctionType
+
+P = 128
+PACK = 4
+K_PASS = P * PACK
+DM = 1024
+PASSES = DM // K_PASS
+H = 8
+D = 128
+PAIRS = D // 2
+HD = H * D
+BANK = 512
+BANK_HEADS = BANK // D
+EPS = 1e-6
+
+TEXT_TILES = 2
+IMAGE_TILES = 6
+TOKEN_TILES = TEXT_TILES + IMAGE_TILES
+STREAM_TILES = ((TEXT_TILES, IMAGE_TILES), (0, TEXT_TILES))
+
+VECTOR_COLS = 512
+
+FLOPS = 2 * (TOKEN_TILES * P) * DM * (2 * HD)
+
+
+def tile_fluxjointattention_pa_kernel(
+    tc,
+    hidden_states,
+    encoder_hidden_states,
+    rope_cos,
+    rope_sin,
+    Wq,
+    Wk,
+    Waq,
+    Wak,
+    bq,
+    bk,
+    baq,
+    bak,
+    g_q,
+    g_k,
+    g_aq,
+    g_ak,
+    out_0,
+    out_1,
+):
+    nc = tc.nc
+    weights = (Wq, Wk, Waq, Wak)
+    biases = (bq, bk, baq, bak)
+    gains = (g_q, g_k, g_aq, g_ak)
+    outs = (out_0, out_1)
+
+    def token_rows(dram_rows, tile_lo, tiles):
+        rows = dram_rows[tile_lo * P : (tile_lo + tiles) * P, :]
+        return rows.rearrange("(p n) c -> p n c", n=tiles)
+
+    with ExitStack() as ctx:
+        keep = ctx.enter_context(tc.tile_pool(name="keep", bufs=1))
+        raw_pool = ctx.enter_context(tc.tile_pool(name="raw", bufs=2))
+        stage = ctx.enter_context(tc.tile_pool(name="stage", bufs=2))
+        work = ctx.enter_context(tc.tile_pool(name="work", bufs=3))
+        psum_t = ctx.enter_context(tc.psum_pool(name="psum_t", bufs=2))
+        psum_rot = ctx.enter_context(tc.psum_pool(name="psum_rot", bufs=2))
+        psum_y = ctx.enter_context(tc.psum_pool(name="psum_y", bufs=4))
+
+        rows = keep.tile([P, 4 * D + 4 * HD], BF16)
+        nc.vector.memset(rows[:].bitcast(I32), 0)
+        act_sb = keep.tile([P, TOKEN_TILES, DM], BF16)
+        cos_sb = keep.tile([P, TOKEN_TILES, D], BF16)
+        sin_sb = keep.tile([P, TOKEN_TILES, D], BF16)
+        image_rows = hidden_states.rearrange("b (p n) k -> p (b n) k", n=IMAGE_TILES)
+        text_rows = encoder_hidden_states.rearrange("b (p n) k -> p (b n) k", n=TEXT_TILES)
+
+        def load_bias(m):
+            nc.sync.dma_start(
+                out=rows[0:1, 4 * D + m * HD : 4 * D + (m + 1) * HD], in_=biases[m].unsqueeze(0)
+            )
+
+        def load_weight(m):
+            raw = raw_pool.tile([P, PASSES, PACK, HD], BF16, name="raw")
+            for g in range(PASSES):
+                nc.sync.dma_start(
+                    out=raw[:, g, :, :].rearrange("p t n -> p (t n)"),
+                    in_=weights[m][g * K_PASS : (g + 1) * K_PASS, :].rearrange("(p t) n -> p (t n)", t=PACK),
+                )
+            return raw
+
+        for m in range(4):
+            nc.sync.dma_start(out=rows[0:1, m * D : (m + 1) * D], in_=gains[m].unsqueeze(0))
+        load_bias(0)
+        nc.sync.dma_start(out=cos_sb[:, TEXT_TILES:, :], in_=token_rows(rope_cos, TEXT_TILES, IMAGE_TILES))
+        nc.sync.dma_start(out=sin_sb[:, TEXT_TILES:, :], in_=token_rows(rope_sin, TEXT_TILES, IMAGE_TILES))
+        nc.sync.dma_start(out=act_sb[:, TEXT_TILES : TEXT_TILES + 2, :], in_=image_rows[:, :2, :])
+        raw_q = load_weight(0)
+        load_bias(1)
+        nc.sync.dma_start(out=act_sb[:, TEXT_TILES + 2 :, :], in_=image_rows[:, 2:, :])
+        raw_k = load_weight(1)
+        nc.sync.dma_start(out=act_sb[:, :TEXT_TILES, :], in_=text_rows)
+        nc.sync.dma_start(out=cos_sb[:, :TEXT_TILES, :], in_=token_rows(rope_cos, 0, TEXT_TILES))
+        nc.sync.dma_start(out=sin_sb[:, :TEXT_TILES, :], in_=token_rows(rope_sin, 0, TEXT_TILES))
+        load_bias(2)
+        load_bias(3)
+
+        ident = keep.tile([P, P], F32)
+        make_identity(nc, ident[:])
+        eps_col = keep.tile([P, 1], F32)
+        nc.vector.memset(eps_col[:], EPS)
+        ones = keep.tile([P, P], BF16)
+        nc.vector.memset(ones[:], 1.0)
+
+        def spread(col_lo):
+            bank = psum_y.tile([P, BANK], F32, name="acc")
+            nc.tensor.matmul(out=bank[:], lhsT=ones[:], rhs=rows[:, col_lo : col_lo + BANK], start=True, stop=True)
+            return bank
+
+        bias_bc = keep.tile([P, 4, H, 2, PAIRS], BF16)
+
+        def spread_bias(m):
+            for bank in range(HD // BANK):
+                nc.scalar.copy(
+                    out=bias_bc[:, m, bank * BANK_HEADS : (bank + 1) * BANK_HEADS, :, :],
+                    in_=spread(4 * D + m * HD + bank * BANK)[:].rearrange(
+                        "p (h i t) -> p h t i", h=BANK_HEADS, t=2
+                    ),
+                )
+
+        gain_pairs = spread(0)[:].rearrange("p (m i t) -> p m i t", m=4, t=2)
+        gain_same = keep.tile([P, 4, 2, PAIRS], F32)
+        gain_other = keep.tile([P, 4, 2, PAIRS], F32)
+        nc.vector.tensor_copy(out=gain_same[:], in_=gain_pairs.rearrange("p m i t -> p m t i"))
+        nc.vector.tensor_scalar_mul(out=gain_other[:, :, 0, :], in0=gain_pairs[:, :, :, 1], scalar1=-1.0)
+        nc.vector.tensor_copy(out=gain_other[:, :, 1, :], in_=gain_pairs[:, :, :, 0])
+
+        SAME, OTHER = 0, 1
+        rot = keep.tile([P, TOKEN_TILES, 2, 2, D], F32)
+
+        def build_tables(stream):
+            tile_lo, tiles = STREAM_TILES[stream]
+            tile_range = slice(tile_lo, tile_lo + tiles)
+            shape = [P, tiles, 2, PAIRS]
+            for qk in range(2):
+                m = 2 * stream + qk
+                nc.vector.tensor_tensor(
+                    out=rot[:, tile_range, qk, SAME, :].rearrange("p n (t i) -> p n t i", t=2),
+                    in0=cos_sb[:, tile_range, :].rearrange("p n (i t) -> p n t i", t=2),
+                    in1=gain_same[:, m, :, :].unsqueeze(1).to_broadcast(shape),
+                    op=ALU.mult,
+                )
+                nc.vector.tensor_tensor(
+                    out=rot[:, tile_range, qk, OTHER, :].rearrange("p n (t i) -> p n t i", t=2),
+                    in0=sin_sb[:, tile_range, :].rearrange("p n (i t) -> p n t i", t=2),
+                    in1=gain_other[:, m, :, :].unsqueeze(1).to_broadcast(shape),
+                    op=ALU.mult,
+                )
+
+        act_words = act_sb[:].bitcast(F32)
+        act_codes = keep.tile([P, PASSES, TOKEN_TILES * P], U32, align_bytes=64)
+        act_scales = keep.tile([P, PASSES, TOKEN_TILES * P], U8, align_bytes=64)
+
+        def quantise_activations(first_tile):
+            grouped = stage.tile([P, PASSES, 2 * P, PACK], BF16, name="act_grouped", align_bytes=64)
+            grouped_words = grouped[:].bitcast(F32)
+            for j in range(2):
+                turned = psum_t.tile([P, PASSES * 2, P], F32, name="turned")
+                for w in range(PASSES * 2):
+                    g, u = divmod(w, 2)
+                    nc.tensor.transpose(
+                        out=turned[:, w, :],
+                        in_=act_words[:, first_tile + j, 2 * P * g + u : 2 * P * (g + 1) : 2],
+                        identity=ident[:],
+                    )
+                nc.scalar.copy(
+                    out=grouped_words[:, :, j * P : (j + 1) * P, :],
+                    in_=turned[:].rearrange("p (g u) r -> p g r u", u=2),
+                )
+            cols = slice(first_tile * P, (first_tile + 2) * P)
+            for g in range(PASSES):
+                nc.vector.quantize_mx(
+                    out=act_codes[:, g, cols].bitcast(FP8X4),
+                    scales=act_scales[:, g, cols],
+                    in_=grouped[:, g, :, :].rearrange("p r j -> p (r j)"),
+                )
+
+        w_codes = keep.tile([P, 4, PASSES, HD], U32, align_bytes=64)
+        w_scales = keep.tile([P, 4, PASSES, HD], U8, align_bytes=64)
+
+        def quantise_weight_pass(raw, m, g):
+            grouped = stage.tile([P, HD, PACK], BF16, name="w_grouped", align_bytes=64)
+            dst = grouped[:].rearrange("p (c i) t -> p c t i", i=4)
+            src = raw[:, g, :, :].rearrange("p t (c i) -> p c t i", i=4)
+            split = VECTOR_COLS // 4
+            nc.vector.tensor_copy(out=dst[:, :split], in_=src[:, :split])
+            nc.scalar.copy(out=dst[:, split:], in_=src[:, split:])
+            for bank in range(HD // BANK):
+                cols = slice(bank * BANK, (bank + 1) * BANK)
+                nc.vector.quantize_mx(
+                    out=w_codes[:, m, g, cols].bitcast(FP8X4),
+                    scales=w_scales[:, m, g, cols],
+                    in_=grouped[:, cols, :].rearrange("p c t -> p (c t)"),
+                )
+
+        units = [(TEXT_TILES + j, 0, qk) for qk in range(2) for j in range(IMAGE_TILES)]
+        units += [(n, 1, qk) for qk in range(2) for n in range(TEXT_TILES)]
+        in_psum = {}
+        in_sbuf = {}
+
+        def multiply(u):
+            n, stream, qk = units[u]
+            m = 2 * stream + qk
+            rot_ps = psum_rot.tile([P, 2, D], F32, name="rot_ps")
+            nc.tensor.matmul(
+                out=rot_ps[:].rearrange("p s d -> p (s d)"),
+                lhsT=ident[:],
+                rhs=rot[:, n, qk, :, :].rearrange("p s d -> p (s d)"),
+                start=True,
+                stop=True,
+            )
+            tokens = slice(n * P, (n + 1) * P)
+            banks = []
+            for bank in range(HD // BANK):
+                cols = slice(bank * BANK, (bank + 1) * BANK)
+                acc = psum_y.tile([P, BANK], F32, name="acc")
+                for g in range(PASSES):
+                    nc.tensor.matmul_mx(
+                        out=acc[:],
+                        lhsT=act_codes[:, g, tokens].bitcast(FP8X4),
+                        lhsT_scale=act_scales[:, g, tokens],
+                        rhs=w_codes[:, m, g, cols].bitcast(FP8X4),
+                        rhs_scale=w_scales[:, m, g, cols],
+                        start=(g == 0),
+                        stop=(g == PASSES - 1),
+                    )
+                banks.append(acc)
+            in_psum[u] = (rot_ps, banks)
+
+        def bias_squares_products(u):
+            n, stream, qk = units[u]
+            m = 2 * stream + qk
+            rot_ps, banks = in_psum[u]
+            y = work.tile([P, H, 2, PAIRS], F32, name="y")
+            for bank in range(HD // BANK):
+                heads = slice(bank * BANK_HEADS, (bank + 1) * BANK_HEADS)
+                nc.vector.tensor_tensor(
+                    out=y[:, heads, :, :],
+                    in0=banks[bank][:].rearrange("p (h i t) -> p h t i", h=BANK_HEADS, t=2),
+                    in1=bias_bc[:, m, heads, :, :],
+                    op=ALU.add,
+                )
+            sumsq = work.tile([P, H], F32, name="sumsq", bufs=4)
+            for h in range(H):
+                squares = work.tile([P, D], BF16, name="squares")
+                nc.scalar.activation(
+                    out=squares[:],
+                    in_=y[:, h, :, :].rearrange("p t i -> p (t i)"),
+                    func=ACT.Square,
+                    accum_out=sumsq[:, h : h + 1],
+                )
+            inv_rms = work.tile([P, H], F32, name="inv_rms", bufs=4)
+            nc.scalar.activation(
+                out=inv_rms[:], in_=sumsq[:], func=ACT.Abs_reciprocal_sqrt, bias=eps_col[:, 0:1], scale=1.0 / D
+            )
+            same = work.tile([P, H, 2, PAIRS], F32, name="same", bufs=4)
+            nc.vector.tensor_tensor(
+                out=same[:].rearrange("p h t i -> p h (t i)"),
+                in0=y[:].rearrange("p h t i -> p h (t i)"),
+                in1=rot_ps[:, SAME, :].unsqueeze(1).to_broadcast([P, H, D]),
+                op=ALU.mult,
+            )
+            other = work.tile([P, H, 2, PAIRS], F32, name="other")
+            nc.vector.tensor_tensor(
+                out=other[:, :, 0, :],
+                in0=y[:, :, 1, :],
+                in1=rot_ps[:, OTHER, :PAIRS].unsqueeze(1).to_broadcast([P, H, PAIRS]),
+                op=ALU.mult,
+            )
+            if stream == 0:
+                nc.gpsimd.tensor_tensor(
+                    out=other[:, :, 1, :],
+                    in0=y[:, :, 0, :],
+                    in1=rot[:, n, qk, OTHER, PAIRS:].unsqueeze(1).to_broadcast([P, H, PAIRS]),
+                    op=ALU.mult,
+                )
+            else:
+                nc.vector.tensor_tensor(
+                    out=other[:, :, 1, :],
+                    in0=y[:, :, 0, :],
+                    in1=rot_ps[:, OTHER, PAIRS:].unsqueeze(1).to_broadcast([P, H, PAIRS]),
+                    op=ALU.mult,
+                )
+            in_sbuf[u] = (same, other, inv_rms)
+
+        def add_products(u):
+            same, other, inv_rms = in_sbuf[u]
+            nc.gpsimd.tensor_tensor(out=same[:], in0=same[:], in1=other[:], op=ALU.add)
+
+        def normalise_store(u):
+            n, stream, qk = units[u]
+            same, other, inv_rms = in_sbuf[u]
+            result = work.tile([P, H, PAIRS, 2], F32, name="result")
+            for h in range(H):
+                nc.scalar.activation(
+                    out=result[:, h, :, :],
+                    in_=same[:, h, :, :].rearrange("p t i -> p i t"),
+                    func=ACT.Copy,
+                    scale=inv_rms[:, h : h + 1],
+                )
+            tile_lo, tiles = STREAM_TILES[stream]
+            out_rows = token_rows(outs[qk].rearrange("b s h d -> (b s) (h d)"), tile_lo, tiles)
+            nc.scalar.dma_start(out=out_rows[:, n - tile_lo, :], in_=result[:].rearrange("p h i t -> p (h i t)"))
+
+        build_tables(0)
+        quantise_activations(TEXT_TILES)
+        for g in range(PASSES):
+            quantise_weight_pass(raw_q, 0, g)
+        spread_bias(0)
+        raws = {1: raw_k, 2: load_weight(2)}
+
+        multiply(0)
+        for s in range(len(units) + 2):
+            if s + 1 < len(units):
+                multiply(s + 1)
+            if 1 <= s <= len(units):
+                add_products(s - 1)
+            if s >= 2:
+                normalise_store(s - 2)
+            if s < len(units):
+                bias_squares_products(s)
+            if s == 0:
+                quantise_activations(TEXT_TILES + 2)
+                quantise_activations(TEXT_TILES + 4)
+            elif s <= 2:
+                quantise_weight_pass(raws[1], 1, s - 1)
+            elif s == 3:
+                raws[3] = load_weight(3)
+                spread_bias(1)
+                quantise_activations(0)
+            elif s <= 5:
+                quantise_weight_pass(raws[2], 2, s - 4)
+            elif s == 6:
+                build_tables(1)
+                spread_bias(2)
+                spread_bias(3)
+            elif s <= 8:
+                quantise_weight_pass(raws[3], 3, s - 7)

@@ -11,6 +11,7 @@ I32 = mybir.dt.int32
 FP8X4 = mybir.dt.float8_e4m3fn_x4
 ALU = mybir.AluOpType
 ACT = mybir.ActivationFunctionType
+AXIS = mybir.AxisListType
 
 P = 128
 PACK = 4
@@ -19,10 +20,8 @@ DM = 1024
 PASSES = DM // K_PASS
 H = 8
 D = 128
-PAIRS = D // 2
 HD = H * D
 BANK = 512
-BANK_HEADS = BANK // D
 EPS = 1e-6
 
 TEXT_TILES = 2
@@ -30,7 +29,9 @@ IMAGE_TILES = 6
 TOKEN_TILES = TEXT_TILES + IMAGE_TILES
 STREAM_TILES = ((TEXT_TILES, IMAGE_TILES), (0, TEXT_TILES))
 
-VECTOR_COLS = 512
+HALF = HD // 2
+SHARE_FIRST = (256, 128, 128)
+SHARE = (192, 128, 192)
 
 FLOPS = 2 * (TOKEN_TILES * P) * DM * (2 * HD)
 
@@ -62,107 +63,116 @@ def tile_fluxjointattention_pa_kernel(
     gains = (g_q, g_k, g_aq, g_ak)
     outs = (out_0, out_1)
 
-    def token_rows(dram_rows, tile_lo, tiles):
+    def token_rows(dram_rows, stream):
+        tile_lo, tiles = STREAM_TILES[stream]
         rows = dram_rows[tile_lo * P : (tile_lo + tiles) * P, :]
         return rows.rearrange("(p n) c -> p n c", n=tiles)
 
     with ExitStack() as ctx:
         keep = ctx.enter_context(tc.tile_pool(name="keep", bufs=1))
-        raw_pool = ctx.enter_context(tc.tile_pool(name="raw", bufs=2))
-        stage = ctx.enter_context(tc.tile_pool(name="stage", bufs=2))
+        raw_pool = ctx.enter_context(tc.tile_pool(name="raw", bufs=4))
+        stage = ctx.enter_context(tc.tile_pool(name="stage", bufs=3))
         work = ctx.enter_context(tc.tile_pool(name="work", bufs=3))
-        psum_t = ctx.enter_context(tc.psum_pool(name="psum_t", bufs=2))
-        psum_rot = ctx.enter_context(tc.psum_pool(name="psum_rot", bufs=2))
-        psum_y = ctx.enter_context(tc.psum_pool(name="psum_y", bufs=4))
+        psum_acc = ctx.enter_context(tc.psum_pool(name="psum_acc", bufs=4))
+        psum_out = ctx.enter_context(tc.psum_pool(name="psum_out", bufs=2))
+        psum_sum = ctx.enter_context(tc.psum_pool(name="psum_sum", bufs=2))
 
-        rows = keep.tile([P, 4 * D + 4 * HD], BF16)
-        nc.vector.memset(rows[:].bitcast(I32), 0)
+        vec_rows = keep.tile([P, P], BF16)
+        nc.gpsimd.memset(vec_rows[:].bitcast(I32), 0)
+        for m in range(4):
+            nc.scalar.dma_start(out=vec_rows[m * H : (m + 1) * H, :], in_=biases[m].rearrange("(h d) -> h d", h=H))
+            nc.scalar.dma_start(out=vec_rows[4 * H + m : 4 * H + m + 1, :], in_=gains[m].unsqueeze(0))
+
         act_sb = keep.tile([P, TOKEN_TILES, DM], BF16)
         cos_sb = keep.tile([P, TOKEN_TILES, D], BF16)
         sin_sb = keep.tile([P, TOKEN_TILES, D], BF16)
         image_rows = hidden_states.rearrange("b (p n) k -> p (b n) k", n=IMAGE_TILES)
         text_rows = encoder_hidden_states.rearrange("b (p n) k -> p (b n) k", n=TEXT_TILES)
 
-        def load_bias(m):
+        def load_tables(stream):
+            tile_lo, tiles = STREAM_TILES[stream]
+            nc.sync.dma_start(out=cos_sb[:, tile_lo : tile_lo + tiles, :], in_=token_rows(rope_cos, stream))
+            nc.sync.dma_start(out=sin_sb[:, tile_lo : tile_lo + tiles, :], in_=token_rows(rope_sin, stream))
+
+        def load_weight(raw, m, g, cols):
             nc.sync.dma_start(
-                out=rows[0:1, 4 * D + m * HD : 4 * D + (m + 1) * HD], in_=biases[m].unsqueeze(0)
+                out=raw[:, g, :, cols],
+                in_=weights[m][g * K_PASS : (g + 1) * K_PASS, cols].rearrange("(p t) n -> p t n", t=PACK),
             )
 
-        def load_weight(m):
-            raw = raw_pool.tile([P, PASSES, PACK, HD], BF16, name="raw")
-            for g in range(PASSES):
-                nc.sync.dma_start(
-                    out=raw[:, g, :, :].rearrange("p t n -> p (t n)"),
-                    in_=weights[m][g * K_PASS : (g + 1) * K_PASS, :].rearrange("(p t) n -> p (t n)", t=PACK),
-                )
-            return raw
-
+        raws = []
         for m in range(4):
-            nc.sync.dma_start(out=rows[0:1, m * D : (m + 1) * D], in_=gains[m].unsqueeze(0))
-        load_bias(0)
-        nc.sync.dma_start(out=cos_sb[:, TEXT_TILES:, :], in_=token_rows(rope_cos, TEXT_TILES, IMAGE_TILES))
-        nc.sync.dma_start(out=sin_sb[:, TEXT_TILES:, :], in_=token_rows(rope_sin, TEXT_TILES, IMAGE_TILES))
-        nc.sync.dma_start(out=act_sb[:, TEXT_TILES : TEXT_TILES + 2, :], in_=image_rows[:, :2, :])
-        raw_q = load_weight(0)
-        load_bias(1)
-        nc.sync.dma_start(out=act_sb[:, TEXT_TILES + 2 :, :], in_=image_rows[:, 2:, :])
-        raw_k = load_weight(1)
+            raw = raw_pool.tile([P, PASSES, PACK, HD], BF16, name="raw")
+            raws.append(raw)
+        load_tables(0)
+        nc.sync.dma_start(out=act_sb[:, TEXT_TILES : TEXT_TILES + 4, :], in_=image_rows[:, :4, :])
+        for g in range(PASSES):
+            load_weight(raws[0], 0, g, slice(0, HALF))
+        nc.sync.dma_start(out=act_sb[:, TEXT_TILES + 4 :, :], in_=image_rows[:, 4:, :])
+        for g in range(PASSES):
+            load_weight(raws[0], 0, g, slice(HALF, HD))
+        for g in range(PASSES):
+            load_weight(raws[1], 1, g, slice(0, HD))
         nc.sync.dma_start(out=act_sb[:, :TEXT_TILES, :], in_=text_rows)
-        nc.sync.dma_start(out=cos_sb[:, :TEXT_TILES, :], in_=token_rows(rope_cos, 0, TEXT_TILES))
-        nc.sync.dma_start(out=sin_sb[:, :TEXT_TILES, :], in_=token_rows(rope_sin, 0, TEXT_TILES))
-        load_bias(2)
-        load_bias(3)
+        load_tables(1)
+        for m in (2, 3):
+            for g in range(PASSES):
+                load_weight(raws[m], m, g, slice(0, HD))
 
         ident = keep.tile([P, P], F32)
         make_identity(nc, ident[:])
+        ident_bf = keep.tile([P, P], BF16)
+        nc.vector.tensor_copy(out=ident_bf[:], in_=ident[:])
+        flip = keep.tile([P, P], F32)
+        ident_pairs = ident[:].rearrange("p (i t) -> p t i", t=2)
+        flip_pairs = flip[:].rearrange("p (i t) -> p t i", t=2)
+        for t in range(2):
+            nc.vector.tensor_copy(out=flip_pairs[:, t, :], in_=ident_pairs[:, 1 - t, :])
+        parity = keep.tile([P, 2], F32)
+        nc.vector.tensor_reduce(out=parity[:], in_=ident_pairs, axis=AXIS.X, op=ALU.add)
+        sign = keep.tile([P, 1], F32)
+        nc.vector.tensor_sub(out=sign[:], in0=parity[:, 0:1], in1=parity[:, 1:2])
         eps_col = keep.tile([P, 1], F32)
         nc.vector.memset(eps_col[:], EPS)
-        ones = keep.tile([P, P], BF16)
+        ones = keep.tile([P, 2], F32)
         nc.vector.memset(ones[:], 1.0)
 
-        def spread(col_lo):
-            bank = psum_y.tile([P, BANK], F32, name="acc")
-            nc.tensor.matmul(out=bank[:], lhsT=ones[:], rhs=rows[:, col_lo : col_lo + BANK], start=True, stop=True)
-            return bank
+        vec_ps = psum_out.tile([P, P], BF16, name="turned")
+        nc.tensor.transpose(out=vec_ps[:], in_=vec_rows[:], identity=ident_bf[:])
+        vec_cols = keep.tile([P, 4 * H + 4], F32)
+        nc.vector.tensor_copy(out=vec_cols[:], in_=vec_ps[:, : 4 * H + 4])
+        signed_gain = keep.tile([P, 4], F32)
+        nc.vector.tensor_scalar_mul(out=signed_gain[:], in0=vec_cols[:, 4 * H :], scalar1=sign[:, 0:1])
 
-        bias_bc = keep.tile([P, 4, H, 2, PAIRS], BF16)
-
-        def spread_bias(m):
-            for bank in range(HD // BANK):
-                nc.scalar.copy(
-                    out=bias_bc[:, m, bank * BANK_HEADS : (bank + 1) * BANK_HEADS, :, :],
-                    in_=spread(4 * D + m * HD + bank * BANK)[:].rearrange(
-                        "p (h i t) -> p h t i", h=BANK_HEADS, t=2
-                    ),
-                )
-
-        gain_pairs = spread(0)[:].rearrange("p (m i t) -> p m i t", m=4, t=2)
-        gain_same = keep.tile([P, 4, 2, PAIRS], F32)
-        gain_other = keep.tile([P, 4, 2, PAIRS], F32)
-        nc.vector.tensor_copy(out=gain_same[:], in_=gain_pairs.rearrange("p m i t -> p m t i"))
-        nc.vector.tensor_scalar_mul(out=gain_other[:, :, 0, :], in0=gain_pairs[:, :, :, 1], scalar1=-1.0)
-        nc.vector.tensor_copy(out=gain_other[:, :, 1, :], in_=gain_pairs[:, :, :, 0])
-
-        SAME, OTHER = 0, 1
-        rot = keep.tile([P, TOKEN_TILES, 2, 2, D], F32)
+        sin_swapped = keep.tile([P, TOKEN_TILES, D], BF16)
+        cos_table = keep.tile([P, 2, TOKEN_TILES * P], F32)
+        sin_table = keep.tile([P, 2, TOKEN_TILES * P], F32)
 
         def build_tables(stream):
             tile_lo, tiles = STREAM_TILES[stream]
             tile_range = slice(tile_lo, tile_lo + tiles)
-            shape = [P, tiles, 2, PAIRS]
+            cols = slice(tile_lo * P, (tile_lo + tiles) * P)
+            swapped_pairs = sin_swapped[:, tile_range, :].rearrange("p n (i t) -> p n t i", t=2)
+            sin_pairs = sin_sb[:, tile_range, :].rearrange("p n (i t) -> p n t i", t=2)
+            for t in range(2):
+                nc.vector.tensor_copy(out=swapped_pairs[:, :, t, :], in_=sin_pairs[:, :, 1 - t, :])
+            cos_ps = psum_out.tile([P, tiles * P], BF16, name="turned")
+            sin_ps = psum_out.tile([P, tiles * P], BF16, name="turned")
+            for source, bank in ((cos_sb, cos_ps), (sin_swapped, sin_ps)):
+                for j in range(tiles):
+                    nc.tensor.transpose(
+                        out=bank[:, j * P : (j + 1) * P], in_=source[:, tile_lo + j, :], identity=ident_bf[:]
+                    )
             for qk in range(2):
                 m = 2 * stream + qk
-                nc.vector.tensor_tensor(
-                    out=rot[:, tile_range, qk, SAME, :].rearrange("p n (t i) -> p n t i", t=2),
-                    in0=cos_sb[:, tile_range, :].rearrange("p n (i t) -> p n t i", t=2),
-                    in1=gain_same[:, m, :, :].unsqueeze(1).to_broadcast(shape),
-                    op=ALU.mult,
+                nc.scalar.activation(
+                    out=cos_table[:, qk, cols],
+                    in_=cos_ps[:],
+                    func=ACT.Copy,
+                    scale=vec_cols[:, 4 * H + m : 4 * H + m + 1],
                 )
-                nc.vector.tensor_tensor(
-                    out=rot[:, tile_range, qk, OTHER, :].rearrange("p n (t i) -> p n t i", t=2),
-                    in0=sin_sb[:, tile_range, :].rearrange("p n (i t) -> p n t i", t=2),
-                    in1=gain_other[:, m, :, :].unsqueeze(1).to_broadcast(shape),
-                    op=ALU.mult,
+                nc.vector.tensor_scalar_mul(
+                    out=sin_table[:, qk, cols], in0=sin_ps[:], scalar1=signed_gain[:, m : m + 1]
                 )
 
         act_words = act_sb[:].bitcast(F32)
@@ -173,18 +183,20 @@ def tile_fluxjointattention_pa_kernel(
             grouped = stage.tile([P, PASSES, 2 * P, PACK], BF16, name="act_grouped", align_bytes=64)
             grouped_words = grouped[:].bitcast(F32)
             for j in range(2):
-                turned = psum_t.tile([P, PASSES * 2, P], F32, name="turned")
-                for w in range(PASSES * 2):
-                    g, u = divmod(w, 2)
-                    nc.tensor.transpose(
-                        out=turned[:, w, :],
-                        in_=act_words[:, first_tile + j, 2 * P * g + u : 2 * P * (g + 1) : 2],
-                        identity=ident[:],
-                    )
-                nc.scalar.copy(
-                    out=grouped_words[:, :, j * P : (j + 1) * P, :],
-                    in_=turned[:].rearrange("p (g u) r -> p g r u", u=2),
-                )
+                turned = psum_acc.tile([P, PASSES, 2, P], F32, name="acc")
+                for g in range(PASSES):
+                    for u in range(2):
+                        nc.tensor.transpose(
+                            out=turned[:, g, u, :],
+                            in_=act_words[:, first_tile + j, 2 * P * g + u : 2 * P * (g + 1) : 2],
+                            identity=ident[:],
+                        )
+                target = grouped_words[:, :, j * P : (j + 1) * P, :]
+                source = turned[:].rearrange("p g u r -> p g r u")
+                if j == 0:
+                    nc.scalar.copy(out=target, in_=source)
+                else:
+                    nc.vector.tensor_copy(out=target, in_=source)
             cols = slice(first_tile * P, (first_tile + 2) * P)
             for g in range(PASSES):
                 nc.vector.quantize_mx(
@@ -196,161 +208,173 @@ def tile_fluxjointattention_pa_kernel(
         w_codes = keep.tile([P, 4, PASSES, HD], U32, align_bytes=64)
         w_scales = keep.tile([P, 4, PASSES, HD], U8, align_bytes=64)
 
-        def quantise_weight_pass(raw, m, g):
-            grouped = stage.tile([P, HD, PACK], BF16, name="w_grouped", align_bytes=64)
+        def quantise_weight(m, g, half, share):
+            cols = slice(half * HALF, (half + 1) * HALF)
+            grouped = stage.tile([P, HALF, PACK], BF16, name="w_grouped", align_bytes=64)
             dst = grouped[:].rearrange("p (c i) t -> p c t i", i=4)
-            src = raw[:, g, :, :].rearrange("p t (c i) -> p c t i", i=4)
-            split = VECTOR_COLS // 4
-            nc.vector.tensor_copy(out=dst[:, :split], in_=src[:, :split])
-            nc.scalar.copy(out=dst[:, split:], in_=src[:, split:])
-            for bank in range(HD // BANK):
-                cols = slice(bank * BANK, (bank + 1) * BANK)
-                nc.vector.quantize_mx(
-                    out=w_codes[:, m, g, cols].bitcast(FP8X4),
-                    scales=w_scales[:, m, g, cols],
-                    in_=grouped[:, cols, :].rearrange("p c t -> p (c t)"),
-                )
-
-        units = [(TEXT_TILES + j, 0, qk) for qk in range(2) for j in range(IMAGE_TILES)]
-        units += [(n, 1, qk) for qk in range(2) for n in range(TEXT_TILES)]
-        in_psum = {}
-        in_sbuf = {}
-
-        def multiply(u):
-            n, stream, qk = units[u]
-            m = 2 * stream + qk
-            rot_ps = psum_rot.tile([P, 2, D], F32, name="rot_ps")
-            nc.tensor.matmul(
-                out=rot_ps[:].rearrange("p s d -> p (s d)"),
-                lhsT=ident[:],
-                rhs=rot[:, n, qk, :, :].rearrange("p s d -> p (s d)"),
-                start=True,
-                stop=True,
+            src = raws[m][:, g, :, cols].rearrange("p t (c i) -> p c t i", i=4)
+            lo = 0
+            for engine, width in enumerate(share):
+                part = slice(lo // 4, (lo + width) // 4)
+                lo += width
+                if width == 0:
+                    continue
+                if engine == 0:
+                    nc.vector.tensor_copy(out=dst[:, part], in_=src[:, part])
+                elif engine == 1:
+                    nc.scalar.copy(out=dst[:, part], in_=src[:, part])
+                else:
+                    nc.gpsimd.tensor_scalar(
+                        out=dst[:, part], in0=src[:, part], scalar1=1.0, scalar2=0.0, op0=ALU.mult, op1=ALU.add
+                    )
+            nc.vector.quantize_mx(
+                out=w_codes[:, m, g, cols].bitcast(FP8X4),
+                scales=w_scales[:, m, g, cols],
+                in_=grouped[:].rearrange("p c t -> p (c t)"),
             )
-            tokens = slice(n * P, (n + 1) * P)
-            banks = []
-            for bank in range(HD // BANK):
-                cols = slice(bank * BANK, (bank + 1) * BANK)
-                acc = psum_y.tile([P, BANK], F32, name="acc")
+
+        jobs = []
+        for stream in range(2):
+            for qk in range(2):
+                for pair in range(H // 2):
+                    a, b = 2 * pair, 2 * pair + 1
+                    if stream == 0:
+                        jobs.append((stream, qk, pair, ((a, 0, 4),)))
+                        jobs.append((stream, qk, pair, ((b, 0, 4),)))
+                        jobs.append((stream, qk, pair, ((a, 4, 2), (b, 4, 2))))
+                    else:
+                        jobs.append((stream, qk, pair, ((a, 0, 2), (b, 0, 2))))
+        in_psum, in_sbuf, turned_back, results = {}, {}, {}, {}
+
+        def project(u):
+            stream, qk, pair, pieces = jobs[u]
+            m = 2 * stream + qk
+            acc = psum_acc.tile([P, BANK], F32, name="acc")
+            at = 0
+            for head, tile, tiles in pieces:
+                tokens = slice((STREAM_TILES[stream][0] + tile) * P, (STREAM_TILES[stream][0] + tile + tiles) * P)
+                cols = slice(head * D, (head + 1) * D)
                 for g in range(PASSES):
                     nc.tensor.matmul_mx(
-                        out=acc[:],
-                        lhsT=act_codes[:, g, tokens].bitcast(FP8X4),
-                        lhsT_scale=act_scales[:, g, tokens],
-                        rhs=w_codes[:, m, g, cols].bitcast(FP8X4),
-                        rhs_scale=w_scales[:, m, g, cols],
+                        out=acc[:, at : at + tiles * P],
+                        lhsT=w_codes[:, m, g, cols].bitcast(FP8X4),
+                        lhsT_scale=w_scales[:, m, g, cols],
+                        rhs=act_codes[:, g, tokens].bitcast(FP8X4),
+                        rhs_scale=act_scales[:, g, tokens],
                         start=(g == 0),
                         stop=(g == PASSES - 1),
                     )
-                banks.append(acc)
-            in_psum[u] = (rot_ps, banks)
+                at += tiles * P
+            in_psum[u] = acc
 
-        def bias_squares_products(u):
-            n, stream, qk = units[u]
+        def products(u):
+            stream, qk, pair, pieces = jobs[u]
             m = 2 * stream + qk
-            rot_ps, banks = in_psum[u]
-            y = work.tile([P, H, 2, PAIRS], F32, name="y")
-            for bank in range(HD // BANK):
-                heads = slice(bank * BANK_HEADS, (bank + 1) * BANK_HEADS)
-                nc.vector.tensor_tensor(
-                    out=y[:, heads, :, :],
-                    in0=banks[bank][:].rearrange("p (h i t) -> p h t i", h=BANK_HEADS, t=2),
-                    in1=bias_bc[:, m, heads, :, :],
-                    op=ALU.add,
-                )
-            sumsq = work.tile([P, H], F32, name="sumsq", bufs=4)
-            for h in range(H):
-                squares = work.tile([P, D], BF16, name="squares")
-                nc.scalar.activation(
-                    out=squares[:],
-                    in_=y[:, h, :, :].rearrange("p t i -> p (t i)"),
-                    func=ACT.Square,
-                    accum_out=sumsq[:, h : h + 1],
-                )
-            inv_rms = work.tile([P, H], F32, name="inv_rms", bufs=4)
-            nc.scalar.activation(
-                out=inv_rms[:], in_=sumsq[:], func=ACT.Abs_reciprocal_sqrt, bias=eps_col[:, 0:1], scale=1.0 / D
-            )
-            same = work.tile([P, H, 2, PAIRS], F32, name="same", bufs=4)
-            nc.vector.tensor_tensor(
-                out=same[:].rearrange("p h t i -> p h (t i)"),
-                in0=y[:].rearrange("p h t i -> p h (t i)"),
-                in1=rot_ps[:, SAME, :].unsqueeze(1).to_broadcast([P, H, D]),
-                op=ALU.mult,
-            )
-            other = work.tile([P, H, 2, PAIRS], F32, name="other")
-            nc.vector.tensor_tensor(
-                out=other[:, :, 0, :],
-                in0=y[:, :, 1, :],
-                in1=rot_ps[:, OTHER, :PAIRS].unsqueeze(1).to_broadcast([P, H, PAIRS]),
-                op=ALU.mult,
-            )
-            if stream == 0:
-                nc.gpsimd.tensor_tensor(
-                    out=other[:, :, 1, :],
-                    in0=y[:, :, 0, :],
-                    in1=rot[:, n, qk, OTHER, PAIRS:].unsqueeze(1).to_broadcast([P, H, PAIRS]),
-                    op=ALU.mult,
-                )
-            else:
-                nc.vector.tensor_tensor(
-                    out=other[:, :, 1, :],
-                    in0=y[:, :, 0, :],
-                    in1=rot_ps[:, OTHER, PAIRS:].unsqueeze(1).to_broadcast([P, H, PAIRS]),
-                    op=ALU.mult,
-                )
-            in_sbuf[u] = (same, other, inv_rms)
+            acc = in_psum.pop(u)
+            squares = work.tile([P, BANK], F32, name="squares")
+            same = work.tile([P, BANK], F32, name="same")
+            other = work.tile([P, BANK], F32, name="other")
+            at = 0
+            for head, tile, tiles in pieces:
+                part = slice(at, at + tiles * P)
+                tokens = slice((STREAM_TILES[stream][0] + tile) * P, (STREAM_TILES[stream][0] + tile + tiles) * P)
+                bias = vec_cols[:, m * H + head : m * H + head + 1]
+                nc.scalar.activation(out=squares[:, part], in_=acc[:, part], func=ACT.Square, bias=bias)
+                for table, product in ((cos_table, same), (sin_table, other)):
+                    nc.vector.scalar_tensor_tensor(
+                        out=product[:, part],
+                        in0=acc[:, part],
+                        scalar=bias,
+                        in1=table[:, qk, tokens],
+                        op0=ALU.add,
+                        op1=ALU.mult,
+                    )
+                at += tiles * P
+            in_sbuf[u] = (squares, same, other)
 
-        def add_products(u):
-            same, other, inv_rms = in_sbuf[u]
-            nc.gpsimd.tensor_tensor(out=same[:], in0=same[:], in1=other[:], op=ALU.add)
+        def turn(u):
+            squares, same, other = in_sbuf.pop(u)
+            sums = psum_sum.tile([P, 4, 2], F32, name="sums")
+            for j in range(4):
+                nc.tensor.matmul(
+                    out=sums[:, j, :], lhsT=squares[:, j * P : (j + 1) * P], rhs=ones[:], start=True, stop=True
+                )
+            inv_rms = work.tile([P, 4], F32, name="inv_rms")
+            nc.scalar.activation(
+                out=inv_rms[:], in_=sums[:, :, 0], func=ACT.Abs_reciprocal_sqrt, bias=eps_col[:, 0:1], scale=1.0 / D
+            )
+            turned = psum_out.tile([P, 4, D], F32, name="turned")
+            for j in range(4):
+                for product, matrix, first in ((same, ident, True), (other, flip, False)):
+                    nc.tensor.matmul(
+                        out=turned[:, j, :],
+                        lhsT=product[:, j * P : (j + 1) * P],
+                        rhs=matrix[:],
+                        is_transpose=True,
+                        start=first,
+                        stop=not first,
+                    )
+            turned_back[u] = (inv_rms, turned)
 
         def normalise_store(u):
-            n, stream, qk = units[u]
-            same, other, inv_rms = in_sbuf[u]
-            result = work.tile([P, H, PAIRS, 2], F32, name="result")
-            for h in range(H):
-                nc.scalar.activation(
-                    out=result[:, h, :, :],
-                    in_=same[:, h, :, :].rearrange("p t i -> p i t"),
-                    func=ACT.Copy,
-                    scale=inv_rms[:, h : h + 1],
+            stream, qk, pair, pieces = jobs[u]
+            inv_rms, turned = turned_back.pop(u)
+            tiles_all = STREAM_TILES[stream][1]
+            if (stream, qk, pair) not in results:
+                result = work.tile([P, tiles_all, 2, D], F32, name="result")
+                results[(stream, qk, pair)] = result
+            result = results[(stream, qk, pair)]
+            if len(pieces) == 1:
+                head, tile, tiles = pieces[0]
+                for j in range(tiles):
+                    nc.scalar.activation(
+                        out=result[:, tile + j, head % 2, :],
+                        in_=turned[:, j, :],
+                        func=ACT.Copy,
+                        scale=inv_rms[:, j : j + 1],
+                    )
+            else:
+                tile, tiles = pieces[0][1], pieces[0][2]
+                nc.vector.tensor_tensor(
+                    out=result[:, tile : tile + tiles, :, :].rearrange("p j h d -> p h j d"),
+                    in0=turned[:].rearrange("p (h j) d -> p h j d", h=2),
+                    in1=inv_rms[:].rearrange("p (h j) -> p h j", h=2).unsqueeze(3).to_broadcast([P, 2, tiles, D]),
+                    op=ALU.mult,
                 )
-            tile_lo, tiles = STREAM_TILES[stream]
-            out_rows = token_rows(outs[qk].rearrange("b s h d -> (b s) (h d)"), tile_lo, tiles)
-            nc.scalar.dma_start(out=out_rows[:, n - tile_lo, :], in_=result[:].rearrange("p h i t -> p (h i t)"))
+                out_rows = token_rows(outs[qk].rearrange("b s h d -> (b s) (h d)"), stream)
+                nc.sync.dma_start(
+                    out=out_rows[:, :, 2 * pair * D : 2 * (pair + 1) * D],
+                    in_=result[:].rearrange("p n h d -> p n (h d)"),
+                )
 
         build_tables(0)
         quantise_activations(TEXT_TILES)
+        quantise_activations(TEXT_TILES + 2)
         for g in range(PASSES):
-            quantise_weight_pass(raw_q, 0, g)
-        spread_bias(0)
-        raws = {1: raw_k, 2: load_weight(2)}
+            quantise_weight(0, g, 0, SHARE_FIRST)
+        quantise_activations(TEXT_TILES + 4)
 
-        multiply(0)
-        for s in range(len(units) + 2):
-            if s + 1 < len(units):
-                multiply(s + 1)
-            if 1 <= s <= len(units):
-                add_products(s - 1)
+        preparations = {0: [(0, 0, 1)], 1: [(0, 1, 1)]}
+        step = 3
+        for m in (1, 2, 3):
+            for half in range(2):
+                for g in range(PASSES):
+                    preparations.setdefault(step, []).append((m, g, half))
+                    step += 2
+
+        project(0)
+        for s in range(len(jobs) + 2):
+            if s + 1 < len(jobs):
+                project(s + 1)
+            if 1 <= s <= len(jobs):
+                turn(s - 1)
             if s >= 2:
                 normalise_store(s - 2)
-            if s < len(units):
-                bias_squares_products(s)
-            if s == 0:
-                quantise_activations(TEXT_TILES + 2)
-                quantise_activations(TEXT_TILES + 4)
-            elif s <= 2:
-                quantise_weight_pass(raws[1], 1, s - 1)
-            elif s == 3:
-                raws[3] = load_weight(3)
-                spread_bias(1)
+            if s < len(jobs):
+                products(s)
+            for m, g, half in preparations.get(s, []):
+                quantise_weight(m, g, half, SHARE)
+            if s == 12:
                 quantise_activations(0)
-            elif s <= 5:
-                quantise_weight_pass(raws[2], 2, s - 4)
-            elif s == 6:
+            if s == 14:
                 build_tables(1)
-                spread_bias(2)
-                spread_bias(3)
-            elif s <= 8:
-                quantise_weight_pass(raws[3], 3, s - 7)

@@ -24,6 +24,8 @@ HD = H * D
 BANK = 512
 EPS = 1e-6
 
+SUM_COLS = 64
+
 TEXT_TILES = 2
 IMAGE_TILES = 6
 TOKEN_TILES = TEXT_TILES + IMAGE_TILES
@@ -134,7 +136,7 @@ def tile_fluxjointattention_pa_kernel(
         nc.vector.tensor_sub(out=sign[:], in0=parity[:, 0:1], in1=parity[:, 1:2])
         eps_col = keep.tile([P, 1], F32)
         nc.vector.memset(eps_col[:], EPS)
-        ones = keep.tile([P, 2], F32)
+        ones = keep.tile([P, SUM_COLS], F32)
         nc.vector.memset(ones[:], 1.0)
 
         vec_ps = psum_out.tile([P, P], BF16, name="turned")
@@ -294,7 +296,7 @@ def tile_fluxjointattention_pa_kernel(
 
         def turn(u):
             squares, same, other = in_sbuf.pop(u)
-            sums = psum_sum.tile([P, 4, 2], F32, name="sums")
+            sums = psum_sum.tile([P, 4, SUM_COLS], F32, name="sums")
             for j in range(4):
                 nc.tensor.matmul(
                     out=sums[:, j, :], lhsT=squares[:, j * P : (j + 1) * P], rhs=ones[:], start=True, stop=True

@@ -21,10 +21,9 @@ PASSES = DM // K_PASS
 H = 8
 D = 128
 HD = H * D
+PAIRS = D // 2
 BANK = 512
 EPS = 1e-6
-
-SUM_COLS = 64
 
 TEXT_TILES = 2
 IMAGE_TILES = 6
@@ -33,7 +32,12 @@ STREAM_TILES = ((TEXT_TILES, IMAGE_TILES), (0, TEXT_TILES))
 
 HALF = HD // 2
 SHARE_FIRST = (256, 128, 128)
-SHARE = (192, 128, 192)
+SHARE = (128, 0, 384)
+GPSIMD_COLS = 64
+
+SCALE_ON_VECTOR = (2, 5)
+
+SUM_COLS = 32
 
 FLOPS = 2 * (TOKEN_TILES * P) * DM * (2 * HD)
 
@@ -72,7 +76,7 @@ def tile_fluxjointattention_pa_kernel(
 
     with ExitStack() as ctx:
         keep = ctx.enter_context(tc.tile_pool(name="keep", bufs=1))
-        raw_pool = ctx.enter_context(tc.tile_pool(name="raw", bufs=4))
+        raw_pool = ctx.enter_context(tc.tile_pool(name="raw", bufs=2))
         stage = ctx.enter_context(tc.tile_pool(name="stage", bufs=3))
         work = ctx.enter_context(tc.tile_pool(name="work", bufs=3))
         psum_acc = ctx.enter_context(tc.psum_pool(name="psum_acc", bufs=4))
@@ -81,9 +85,18 @@ def tile_fluxjointattention_pa_kernel(
 
         vec_rows = keep.tile([P, P], BF16)
         nc.gpsimd.memset(vec_rows[:].bitcast(I32), 0)
-        for m in range(4):
+        for m in range(2):
             nc.scalar.dma_start(out=vec_rows[m * H : (m + 1) * H, :], in_=biases[m].rearrange("(h d) -> h d", h=H))
-            nc.scalar.dma_start(out=vec_rows[4 * H + m : 4 * H + m + 1, :], in_=gains[m].unsqueeze(0))
+            nc.scalar.dma_start(out=vec_rows[2 * H + m : 2 * H + m + 1, :], in_=gains[m].unsqueeze(0))
+        text_row = keep.tile([P, 2 * D + 2 * HD], BF16)
+        nc.vector.memset(text_row[:].bitcast(I32), 0)
+
+        def load_text_row():
+            for qk in range(2):
+                nc.sync.dma_start(out=text_row[0:1, qk * D : (qk + 1) * D], in_=gains[2 + qk].unsqueeze(0))
+                nc.sync.dma_start(
+                    out=text_row[0:1, 2 * D + qk * HD : 2 * D + (qk + 1) * HD], in_=biases[2 + qk].unsqueeze(0)
+                )
 
         act_sb = keep.tile([P, TOKEN_TILES, DM], BF16)
         cos_sb = keep.tile([P, TOKEN_TILES, D], BF16)
@@ -106,10 +119,10 @@ def tile_fluxjointattention_pa_kernel(
         for m in range(4):
             raw = raw_pool.tile([P, PASSES, PACK, HD], BF16, name="raw")
             raws.append(raw)
-        load_tables(0)
         nc.sync.dma_start(out=act_sb[:, TEXT_TILES : TEXT_TILES + 4, :], in_=image_rows[:, :4, :])
         for g in range(PASSES):
             load_weight(raws[0], 0, g, slice(0, HALF))
+        load_tables(0)
         nc.sync.dma_start(out=act_sb[:, TEXT_TILES + 4 :, :], in_=image_rows[:, 4:, :])
         for g in range(PASSES):
             load_weight(raws[0], 0, g, slice(HALF, HD))
@@ -117,6 +130,7 @@ def tile_fluxjointattention_pa_kernel(
             load_weight(raws[1], 1, g, slice(0, HD))
         nc.sync.dma_start(out=act_sb[:, :TEXT_TILES, :], in_=text_rows)
         load_tables(1)
+        load_text_row()
         for m in (2, 3):
             for g in range(PASSES):
                 load_weight(raws[m], m, g, slice(0, HD))
@@ -138,51 +152,89 @@ def tile_fluxjointattention_pa_kernel(
         nc.vector.memset(eps_col[:], EPS)
         ones = keep.tile([P, SUM_COLS], F32)
         nc.vector.memset(ones[:], 1.0)
+        ones_bf = keep.tile([P, P], BF16)
+        nc.vector.memset(ones_bf[:], 1.0)
+        warm = keep.tile([P, 1], F32)
+        nc.scalar.activation(out=warm[:], in_=eps_col[:], func=ACT.Abs_reciprocal_sqrt)
 
         vec_ps = psum_out.tile([P, P], BF16, name="turned")
         nc.tensor.transpose(out=vec_ps[:], in_=vec_rows[:], identity=ident_bf[:])
-        vec_cols = keep.tile([P, 4 * H + 4], F32)
-        nc.vector.tensor_copy(out=vec_cols[:], in_=vec_ps[:, : 4 * H + 4])
-        signed_gain = keep.tile([P, 4], F32)
-        nc.vector.tensor_scalar_mul(out=signed_gain[:], in0=vec_cols[:, 4 * H :], scalar1=sign[:, 0:1])
+        vec_cols = keep.tile([P, 2 * H + 2], F32)
+        nc.vector.tensor_copy(out=vec_cols[:], in_=vec_ps[:, : 2 * H + 2])
+        signed_gain = keep.tile([P, 2], F32)
+        nc.vector.tensor_scalar_mul(out=signed_gain[:], in0=vec_cols[:, 2 * H :], scalar1=sign[:, 0:1])
 
-        sin_swapped = keep.tile([P, TOKEN_TILES, D], BF16)
-        cos_table = keep.tile([P, 2, TOKEN_TILES * P], F32)
-        sin_table = keep.tile([P, 2, TOKEN_TILES * P], F32)
+        sin_swapped = keep.tile([P, IMAGE_TILES, D], BF16)
+        cos_table = keep.tile([P, 2, IMAGE_TILES * P], F32)
+        sin_table = keep.tile([P, 2, IMAGE_TILES * P], F32)
+        tables_in_psum = []
 
-        def build_tables(stream):
-            tile_lo, tiles = STREAM_TILES[stream]
-            tile_range = slice(tile_lo, tile_lo + tiles)
-            cols = slice(tile_lo * P, (tile_lo + tiles) * P)
-            swapped_pairs = sin_swapped[:, tile_range, :].rearrange("p n (i t) -> p n t i", t=2)
-            sin_pairs = sin_sb[:, tile_range, :].rearrange("p n (i t) -> p n t i", t=2)
+        def turn_tables():
+            swapped_pairs = sin_swapped[:].rearrange("p n (i t) -> p n t i", t=2)
+            sin_pairs = sin_sb[:, TEXT_TILES:, :].rearrange("p n (i t) -> p n t i", t=2)
             for t in range(2):
                 nc.vector.tensor_copy(out=swapped_pairs[:, :, t, :], in_=sin_pairs[:, :, 1 - t, :])
-            cos_ps = psum_out.tile([P, tiles * P], BF16, name="turned")
-            sin_ps = psum_out.tile([P, tiles * P], BF16, name="turned")
-            for source, bank in ((cos_sb, cos_ps), (sin_swapped, sin_ps)):
-                for j in range(tiles):
+            for source in (cos_sb[:, TEXT_TILES:, :], sin_swapped[:]):
+                bank = psum_out.tile([P, IMAGE_TILES * P], BF16, name="turned")
+                for j in range(IMAGE_TILES):
                     nc.tensor.transpose(
-                        out=bank[:, j * P : (j + 1) * P], in_=source[:, tile_lo + j, :], identity=ident_bf[:]
+                        out=bank[:, j * P : (j + 1) * P], in_=source[:, j, :], identity=ident_bf[:]
                     )
+                tables_in_psum.append(bank)
+
+        def build_tables(qk):
+            cos_ps, sin_ps = tables_in_psum
+            nc.scalar.activation(
+                out=cos_table[:, qk, :], in_=cos_ps[:], func=ACT.Copy, scale=vec_cols[:, 2 * H + qk : 2 * H + qk + 1]
+            )
+            nc.vector.tensor_scalar_mul(out=sin_table[:, qk, :], in0=sin_ps[:], scalar1=signed_gain[:, qk : qk + 1])
+
+        def spread(col_lo, width):
+            bank = psum_sum.tile([P, width], F32, name="sums")
+            nc.tensor.matmul(
+                out=bank[:], lhsT=ones_bf[:], rhs=text_row[:, col_lo : col_lo + width], start=True, stop=True
+            )
+            return bank
+
+        SAME, OTHER = 0, 1
+        text_bias = keep.tile([P, 2, H, 2, PAIRS], BF16)
+        gain_same = keep.tile([P, 2, 2, PAIRS], F32)
+        gain_other = keep.tile([P, 2, 2, PAIRS], F32)
+        text_table = keep.tile([P, TEXT_TILES, 2, 2, D], F32)
+
+        def spread_text_gains():
+            pairs = spread(0, 2 * D)[:].rearrange("p (s i t) -> p s i t", s=2, t=2)
+            nc.vector.tensor_copy(out=gain_same[:], in_=pairs.rearrange("p s i t -> p s t i"))
+            nc.vector.tensor_scalar_mul(out=gain_other[:, :, 0, :], in0=pairs[:, :, :, 1], scalar1=-1.0)
+            nc.vector.tensor_copy(out=gain_other[:, :, 1, :], in_=pairs[:, :, :, 0])
+
+        def spread_text_bias(qk):
+            for bank in range(HD // BANK):
+                heads = slice(bank * BANK // D, (bank + 1) * BANK // D)
+                nc.scalar.copy(
+                    out=text_bias[:, qk, heads, :, :],
+                    in_=spread(2 * D + qk * HD + bank * BANK, BANK)[:].rearrange(
+                        "p (h i t) -> p h t i", t=2, h=BANK // D
+                    ),
+                )
+
+        def build_text_tables():
+            shape = [P, TEXT_TILES, 2, PAIRS]
             for qk in range(2):
-                m = 2 * stream + qk
-                nc.scalar.activation(
-                    out=cos_table[:, qk, cols],
-                    in_=cos_ps[:],
-                    func=ACT.Copy,
-                    scale=vec_cols[:, 4 * H + m : 4 * H + m + 1],
-                )
-                nc.vector.tensor_scalar_mul(
-                    out=sin_table[:, qk, cols], in0=sin_ps[:], scalar1=signed_gain[:, m : m + 1]
-                )
+                for which, source, gain in ((SAME, cos_sb, gain_same), (OTHER, sin_sb, gain_other)):
+                    nc.vector.tensor_tensor(
+                        out=text_table[:, :, qk, which, :].rearrange("p n (t i) -> p n t i", t=2),
+                        in0=source[:, :TEXT_TILES, :].rearrange("p n (i t) -> p n t i", t=2),
+                        in1=gain[:, qk, :, :].unsqueeze(1).to_broadcast(shape),
+                        op=ALU.mult,
+                    )
 
         act_words = act_sb[:].bitcast(F32)
         act_codes = keep.tile([P, PASSES, TOKEN_TILES * P], U32, align_bytes=64)
         act_scales = keep.tile([P, PASSES, TOKEN_TILES * P], U8, align_bytes=64)
 
         def quantise_activations(first_tile):
-            grouped = stage.tile([P, PASSES, 2 * P, PACK], BF16, name="act_grouped", align_bytes=64)
+            grouped = stage.tile([P, PASSES, 2 * P, PACK], BF16, name="act_grouped", align_bytes=64, bufs=2)
             grouped_words = grouped[:].bitcast(F32)
             for j in range(2):
                 turned = psum_acc.tile([P, PASSES, 2, P], F32, name="acc")
@@ -210,9 +262,11 @@ def tile_fluxjointattention_pa_kernel(
         w_codes = keep.tile([P, 4, PASSES, HD], U32, align_bytes=64)
         w_scales = keep.tile([P, 4, PASSES, HD], U8, align_bytes=64)
 
-        def quantise_weight(m, g, half, share):
+        regrouped = {}
+
+        def regroup_weight(m, g, half, share):
             cols = slice(half * HALF, (half + 1) * HALF)
-            grouped = stage.tile([P, HALF, PACK], BF16, name="w_grouped", align_bytes=64)
+            grouped = stage.tile([P, HALF, PACK], BF16, name="w_grouped", align_bytes=64, bufs=4)
             dst = grouped[:].rearrange("p (c i) t -> p c t i", i=4)
             src = raws[m][:, g, :, cols].rearrange("p t (c i) -> p c t i", i=4)
             lo = 0
@@ -226,41 +280,48 @@ def tile_fluxjointattention_pa_kernel(
                 elif engine == 1:
                     nc.scalar.copy(out=dst[:, part], in_=src[:, part])
                 else:
-                    nc.gpsimd.tensor_scalar(
-                        out=dst[:, part], in0=src[:, part], scalar1=1.0, scalar2=0.0, op0=ALU.mult, op1=ALU.add
-                    )
+                    for c in range(lo - width, lo, GPSIMD_COLS):
+                        nc.gpsimd.tensor_scalar(
+                            out=grouped[:, c : c + GPSIMD_COLS, :],
+                            in0=raws[m][:, g, :, half * HALF + c : half * HALF + c + GPSIMD_COLS].rearrange(
+                                "p t c -> p c t"
+                            ),
+                            scalar1=1.0,
+                            scalar2=0.0,
+                            op0=ALU.mult,
+                            op1=ALU.add,
+                        )
+            regrouped[(m, g, half)] = grouped
+
+        def quantise_weight(m, g, half):
+            cols = slice(half * HALF, (half + 1) * HALF)
             nc.vector.quantize_mx(
                 out=w_codes[:, m, g, cols].bitcast(FP8X4),
                 scales=w_scales[:, m, g, cols],
-                in_=grouped[:].rearrange("p c t -> p (c t)"),
+                in_=regrouped.pop((m, g, half))[:].rearrange("p c t -> p (c t)"),
             )
 
         jobs = []
-        for stream in range(2):
-            for qk in range(2):
-                for pair in range(H // 2):
-                    a, b = 2 * pair, 2 * pair + 1
-                    if stream == 0:
-                        jobs.append((stream, qk, pair, ((a, 0, 4),)))
-                        jobs.append((stream, qk, pair, ((b, 0, 4),)))
-                        jobs.append((stream, qk, pair, ((a, 4, 2), (b, 4, 2))))
-                    else:
-                        jobs.append((stream, qk, pair, ((a, 0, 2), (b, 0, 2))))
-        in_psum, in_sbuf, turned_back, results = {}, {}, {}, {}
+        for qk in range(2):
+            for pair in range(H // 2):
+                a, b = 2 * pair, 2 * pair + 1
+                jobs.append((qk, pair, ((a, 0, 4),)))
+                jobs.append((qk, pair, ((b, 0, 4),)))
+                jobs.append((qk, pair, ((a, 4, 2), (b, 4, 2))))
+        in_psum, squared, in_sbuf, turned_back, results = {}, {}, {}, {}, {}
 
         def project(u):
-            stream, qk, pair, pieces = jobs[u]
-            m = 2 * stream + qk
+            qk, pair, pieces = jobs[u]
             acc = psum_acc.tile([P, BANK], F32, name="acc")
             at = 0
             for head, tile, tiles in pieces:
-                tokens = slice((STREAM_TILES[stream][0] + tile) * P, (STREAM_TILES[stream][0] + tile + tiles) * P)
+                tokens = slice((TEXT_TILES + tile) * P, (TEXT_TILES + tile + tiles) * P)
                 cols = slice(head * D, (head + 1) * D)
                 for g in range(PASSES):
                     nc.tensor.matmul_mx(
                         out=acc[:, at : at + tiles * P],
-                        lhsT=w_codes[:, m, g, cols].bitcast(FP8X4),
-                        lhsT_scale=w_scales[:, m, g, cols],
+                        lhsT=w_codes[:, qk, g, cols].bitcast(FP8X4),
+                        lhsT_scale=w_scales[:, qk, g, cols],
                         rhs=act_codes[:, g, tokens].bitcast(FP8X4),
                         rhs_scale=act_scales[:, g, tokens],
                         start=(g == 0),
@@ -269,19 +330,31 @@ def tile_fluxjointattention_pa_kernel(
                 at += tiles * P
             in_psum[u] = acc
 
-        def products(u):
-            stream, qk, pair, pieces = jobs[u]
-            m = 2 * stream + qk
-            acc = in_psum.pop(u)
+        def square(u):
+            qk, pair, pieces = jobs[u]
             squares = work.tile([P, BANK], F32, name="squares")
+            at = 0
+            for head, tile, tiles in pieces:
+                part = slice(at, at + tiles * P)
+                nc.scalar.activation(
+                    out=squares[:, part],
+                    in_=in_psum[u][:, part],
+                    func=ACT.Square,
+                    bias=vec_cols[:, qk * H + head : qk * H + head + 1],
+                )
+                at += tiles * P
+            squared[u] = squares
+
+        def products(u):
+            qk, pair, pieces = jobs[u]
+            acc = in_psum.pop(u)
             same = work.tile([P, BANK], F32, name="same")
             other = work.tile([P, BANK], F32, name="other")
             at = 0
             for head, tile, tiles in pieces:
                 part = slice(at, at + tiles * P)
-                tokens = slice((STREAM_TILES[stream][0] + tile) * P, (STREAM_TILES[stream][0] + tile + tiles) * P)
-                bias = vec_cols[:, m * H + head : m * H + head + 1]
-                nc.scalar.activation(out=squares[:, part], in_=acc[:, part], func=ACT.Square, bias=bias)
+                tokens = slice(tile * P, (tile + tiles) * P)
+                bias = vec_cols[:, qk * H + head : qk * H + head + 1]
                 for table, product in ((cos_table, same), (sin_table, other)):
                     nc.vector.scalar_tensor_tensor(
                         out=product[:, part],
@@ -292,7 +365,7 @@ def tile_fluxjointattention_pa_kernel(
                         op1=ALU.mult,
                     )
                 at += tiles * P
-            in_sbuf[u] = (squares, same, other)
+            in_sbuf[u] = (squared.pop(u), same, other)
 
         def turn(u):
             squares, same, other = in_sbuf.pop(u)
@@ -319,64 +392,195 @@ def tile_fluxjointattention_pa_kernel(
             turned_back[u] = (inv_rms, turned)
 
         def normalise_store(u):
-            stream, qk, pair, pieces = jobs[u]
+            qk, pair, pieces = jobs[u]
             inv_rms, turned = turned_back.pop(u)
-            tiles_all = STREAM_TILES[stream][1]
-            if (stream, qk, pair) not in results:
-                result = work.tile([P, tiles_all, 2, D], F32, name="result")
-                results[(stream, qk, pair)] = result
-            result = results[(stream, qk, pair)]
-            if len(pieces) == 1:
-                head, tile, tiles = pieces[0]
-                for j in range(tiles):
-                    nc.scalar.activation(
-                        out=result[:, tile + j, head % 2, :],
-                        in_=turned[:, j, :],
-                        func=ACT.Copy,
-                        scale=inv_rms[:, j : j + 1],
-                    )
-            else:
-                tile, tiles = pieces[0][1], pieces[0][2]
+            if (qk, pair) not in results:
+                result = work.tile([P, IMAGE_TILES, 2, D], F32, name="result")
+                results[(qk, pair)] = result
+            result = results[(qk, pair)]
+            heads = len(pieces)
+            head, tile, tiles = pieces[0]
+            target = result[:, tile : tile + tiles, head % 2 : head % 2 + heads, :].rearrange("p j h d -> p h j d")
+            source = turned[:].rearrange("p (h j) d -> p h j d", h=heads)
+            if u % 8 in SCALE_ON_VECTOR:
                 nc.vector.tensor_tensor(
-                    out=result[:, tile : tile + tiles, :, :].rearrange("p j h d -> p h j d"),
-                    in0=turned[:].rearrange("p (h j) d -> p h j d", h=2),
-                    in1=inv_rms[:].rearrange("p (h j) -> p h j", h=2).unsqueeze(3).to_broadcast([P, 2, tiles, D]),
+                    out=target,
+                    in0=source,
+                    in1=inv_rms[:]
+                    .rearrange("p (h j) -> p h j", h=heads)
+                    .unsqueeze(3)
+                    .to_broadcast([P, heads, tiles, D]),
                     op=ALU.mult,
                 )
-                out_rows = token_rows(outs[qk].rearrange("b s h d -> (b s) (h d)"), stream)
+            else:
+                for h in range(heads):
+                    for j in range(tiles):
+                        nc.scalar.activation(
+                            out=target[:, h, j, :],
+                            in_=source[:, h, j, :],
+                            func=ACT.Copy,
+                            scale=inv_rms[:, h * tiles + j : h * tiles + j + 1],
+                        )
+            if heads == 2:
+                out_rows = token_rows(outs[qk].rearrange("b s h d -> (b s) (h d)"), 0)
                 nc.sync.dma_start(
                     out=out_rows[:, :, 2 * pair * D : 2 * (pair + 1) * D],
                     in_=result[:].rearrange("p n h d -> p n (h d)"),
                 )
 
-        build_tables(0)
+        text_state = {}
+
+        def text_project(job):
+            qk, n = job
+            m = 2 + qk
+            table_ps = psum_sum.tile([P, 2, D], F32, name="sums")
+            nc.tensor.matmul(
+                out=table_ps[:].rearrange("p s d -> p (s d)"),
+                lhsT=ident[:],
+                rhs=text_table[:, n, qk, :, :].rearrange("p s d -> p (s d)"),
+                start=True,
+                stop=True,
+            )
+            tokens = slice(n * P, (n + 1) * P)
+            banks = []
+            for bank in range(HD // BANK):
+                cols = slice(bank * BANK, (bank + 1) * BANK)
+                acc = psum_acc.tile([P, BANK], F32, name="acc")
+                for g in range(PASSES):
+                    nc.tensor.matmul_mx(
+                        out=acc[:],
+                        lhsT=act_codes[:, g, tokens].bitcast(FP8X4),
+                        lhsT_scale=act_scales[:, g, tokens],
+                        rhs=w_codes[:, m, g, cols].bitcast(FP8X4),
+                        rhs_scale=w_scales[:, m, g, cols],
+                        start=(g == 0),
+                        stop=(g == PASSES - 1),
+                    )
+                banks.append(acc)
+            text_state[job] = (table_ps, banks)
+
+        def text_products(job):
+            qk, n = job
+            table_ps, banks = text_state[job]
+            y = work.tile([P, H, 2, PAIRS], F32, name="y", bufs=2)
+            for bank in range(HD // BANK):
+                heads = slice(bank * BANK // D, (bank + 1) * BANK // D)
+                nc.vector.tensor_tensor(
+                    out=y[:, heads, :, :],
+                    in0=banks[bank][:].rearrange("p (h i t) -> p h t i", t=2, h=BANK // D),
+                    in1=text_bias[:, qk, heads, :, :],
+                    op=ALU.add,
+                )
+            sumsq = work.tile([P, H], F32, name="sumsq")
+            for h in range(H):
+                text_squares = work.tile([P, D], BF16, name="text_squares")
+                nc.scalar.activation(
+                    out=text_squares[:],
+                    in_=y[:, h, :, :].rearrange("p t i -> p (t i)"),
+                    func=ACT.Square,
+                    accum_out=sumsq[:, h : h + 1],
+                )
+            text_inv = work.tile([P, H], F32, name="text_inv")
+            nc.scalar.activation(
+                out=text_inv[:], in_=sumsq[:], func=ACT.Abs_reciprocal_sqrt, bias=eps_col[:, 0:1], scale=1.0 / D
+            )
+            text_same = work.tile([P, H, 2, PAIRS], F32, name="text_same", bufs=2)
+            nc.vector.tensor_tensor(
+                out=text_same[:].rearrange("p h t i -> p h (t i)"),
+                in0=y[:].rearrange("p h t i -> p h (t i)"),
+                in1=table_ps[:, SAME, :].unsqueeze(1).to_broadcast([P, H, D]),
+                op=ALU.mult,
+            )
+            text_other = work.tile([P, H, 2, PAIRS], F32, name="text_other", bufs=2)
+            nc.vector.tensor_tensor(
+                out=text_other[:, :, 0, :],
+                in0=y[:, :, 1, :],
+                in1=table_ps[:, OTHER, :PAIRS].unsqueeze(1).to_broadcast([P, H, PAIRS]),
+                op=ALU.mult,
+            )
+            nc.gpsimd.tensor_tensor(
+                out=text_other[:, :, 1, :],
+                in0=y[:, :, 0, :],
+                in1=text_table[:, n, qk, OTHER, PAIRS:].unsqueeze(1).to_broadcast([P, H, PAIRS]),
+                op=ALU.mult,
+            )
+            text_state[job] = (text_same, text_other, text_inv)
+
+        def text_add(job):
+            text_same, text_other, text_inv = text_state[job]
+            nc.gpsimd.tensor_tensor(out=text_same[:], in0=text_same[:], in1=text_other[:], op=ALU.add)
+
+        def text_finish(job):
+            qk, n = job
+            text_same, text_other, text_inv = text_state.pop(job)
+            text_result = work.tile([P, H, PAIRS, 2], F32, name="text_result", bufs=2)
+            for h in range(H):
+                nc.scalar.activation(
+                    out=text_result[:, h, :, :],
+                    in_=text_same[:, h, :, :].rearrange("p t i -> p i t"),
+                    func=ACT.Copy,
+                    scale=text_inv[:, h : h + 1],
+                )
+            out_rows = token_rows(outs[qk].rearrange("b s h d -> (b s) (h d)"), 1)
+            nc.sync.dma_start(
+                out=out_rows[:, n, :], in_=text_result[:].rearrange("p h i t -> p (h i t)")
+            )
+
         quantise_activations(TEXT_TILES)
         quantise_activations(TEXT_TILES + 2)
         for g in range(PASSES):
-            quantise_weight(0, g, 0, SHARE_FIRST)
+            regroup_weight(0, g, 0, SHARE_FIRST)
+        turn_tables()
+        for g in range(PASSES):
+            quantise_weight(0, g, 0)
+        build_tables(0)
+        build_tables(1)
         quantise_activations(TEXT_TILES + 4)
+        for g in range(PASSES):
+            regroup_weight(0, g, 1, SHARE_FIRST)
 
-        preparations = {0: [(0, 0, 1)], 1: [(0, 1, 1)]}
-        step = 3
-        for m in (1, 2, 3):
-            for half in range(2):
-                for g in range(PASSES):
-                    preparations.setdefault(step, []).append((m, g, half))
-                    step += 2
+        pieces_due = [(m, g, half) for m in (1, 2, 3) for half in range(2) for g in range(PASSES)]
+        regroup_at = {i * 3 // 2: piece for i, piece in enumerate(pieces_due)}
 
-        project(0)
-        for s in range(len(jobs) + 2):
-            if s + 1 < len(jobs):
-                project(s + 1)
-            if 1 <= s <= len(jobs):
-                turn(s - 1)
-            if s >= 2:
-                normalise_store(s - 2)
-            if s < len(jobs):
-                products(s)
-            for m, g, half in preparations.get(s, []):
-                quantise_weight(m, g, half, SHARE)
-            if s == 12:
+        IMAGE, TEXT = 0, 1
+        order = [(IMAGE, u) for u in range(len(jobs))]
+        for at, text_job in ((17, (0, 0)), (20, (0, 1)), (23, (1, 0)), (26, (1, 1))):
+            order.insert(at, (TEXT, text_job))
+
+        PROJECT, SQUARE, PRODUCTS, TURN, FINISH = range(5)
+        stages = (
+            (project, text_project),
+            (square, None),
+            (products, text_products),
+            (turn, text_add),
+            (normalise_store, text_finish),
+        )
+
+        def run(stage, at):
+            if 0 <= at < len(order):
+                kind, job = order[at]
+                if stages[stage][kind] is not None:
+                    stages[stage][kind](job)
+
+        run(PROJECT, 0)
+        run(PROJECT, 1)
+        run(SQUARE, 0)
+        for s in range(len(order) + 2):
+            run(TURN, s - 1)
+            run(PROJECT, s + 2)
+            run(SQUARE, s + 1)
+            run(PRODUCTS, s)
+            run(FINISH, s - 2)
+            if s < PASSES:
+                quantise_weight(0, s, 1)
+            if s in regroup_at:
+                regroup_weight(*regroup_at[s], SHARE)
+            if s - 4 in regroup_at:
+                quantise_weight(*regroup_at[s - 4])
+            if s == 6:
                 quantise_activations(0)
-            if s == 14:
-                build_tables(1)
+            if s == 9:
+                spread_text_gains()
+                spread_text_bias(0)
+                spread_text_bias(1)
+                build_text_tables()

@@ -31,13 +31,13 @@ TOKEN_TILES = TEXT_TILES + IMAGE_TILES
 STREAM_TILES = ((TEXT_TILES, IMAGE_TILES), (0, TEXT_TILES))
 
 HALF = HD // 2
-SHARE_FIRST = (256, 128, 128)
-SHARE = (128, 0, 384)
+SHARE_FIRST = (320, 192, 0)
+SHARE = (192, 320, 0)
 GPSIMD_COLS = 64
 
 SCALE_ON_VECTOR = (2, 5)
 
-SUM_COLS = 32
+SUM_COLS = 64
 
 FLOPS = 2 * (TOKEN_TILES * P) * DM * (2 * HD)
 
@@ -157,16 +157,18 @@ def tile_fluxjointattention_pa_kernel(
         warm = keep.tile([P, 1], F32)
         nc.scalar.activation(out=warm[:], in_=eps_col[:], func=ACT.Abs_reciprocal_sqrt)
 
-        vec_ps = psum_out.tile([P, P], BF16, name="turned")
-        nc.tensor.transpose(out=vec_ps[:], in_=vec_rows[:], identity=ident_bf[:])
         vec_cols = keep.tile([P, 2 * H + 2], F32)
-        nc.vector.tensor_copy(out=vec_cols[:], in_=vec_ps[:, : 2 * H + 2])
         signed_gain = keep.tile([P, 2], F32)
-        nc.vector.tensor_scalar_mul(out=signed_gain[:], in0=vec_cols[:, 2 * H :], scalar1=sign[:, 0:1])
 
+        def turn_vectors():
+            vec_ps = psum_sum.tile([P, P], BF16, name="sums")
+            nc.tensor.transpose(out=vec_ps[:], in_=vec_rows[:], identity=ident_bf[:])
+            nc.vector.tensor_copy(out=vec_cols[:], in_=vec_ps[:, : 2 * H + 2])
+            nc.vector.tensor_scalar_mul(out=signed_gain[:], in0=vec_cols[:, 2 * H :], scalar1=sign[:, 0:1])
+
+        SAME, OTHER = 0, 1
         sin_swapped = keep.tile([P, IMAGE_TILES, D], BF16)
-        cos_table = keep.tile([P, 2, IMAGE_TILES * P], F32)
-        sin_table = keep.tile([P, 2, IMAGE_TILES * P], F32)
+        image_table = keep.tile([P, 2, 2, IMAGE_TILES * P], F32)
         tables_in_psum = []
 
         def turn_tables():
@@ -185,9 +187,9 @@ def tile_fluxjointattention_pa_kernel(
         def build_tables(qk):
             cos_ps, sin_ps = tables_in_psum
             nc.scalar.activation(
-                out=cos_table[:, qk, :], in_=cos_ps[:], func=ACT.Copy, scale=vec_cols[:, 2 * H + qk : 2 * H + qk + 1]
+                out=image_table[:, qk, SAME, :], in_=cos_ps[:], func=ACT.Copy, scale=vec_cols[:, 2 * H + qk : 2 * H + qk + 1]
             )
-            nc.vector.tensor_scalar_mul(out=sin_table[:, qk, :], in0=sin_ps[:], scalar1=signed_gain[:, qk : qk + 1])
+            nc.vector.tensor_scalar_mul(out=image_table[:, qk, OTHER, :], in0=sin_ps[:], scalar1=signed_gain[:, qk : qk + 1])
 
         def spread(col_lo, width):
             bank = psum_sum.tile([P, width], F32, name="sums")
@@ -196,7 +198,6 @@ def tile_fluxjointattention_pa_kernel(
             )
             return bank
 
-        SAME, OTHER = 0, 1
         text_bias = keep.tile([P, 2, H, 2, PAIRS], BF16)
         gain_same = keep.tile([P, 2, 2, PAIRS], F32)
         gain_other = keep.tile([P, 2, 2, PAIRS], F32)
@@ -348,27 +349,25 @@ def tile_fluxjointattention_pa_kernel(
         def products(u):
             qk, pair, pieces = jobs[u]
             acc = in_psum.pop(u)
-            same = work.tile([P, BANK], F32, name="same")
-            other = work.tile([P, BANK], F32, name="other")
+            both = work.tile([P, 2, BANK], F32, name="both")
             at = 0
             for head, tile, tiles in pieces:
                 part = slice(at, at + tiles * P)
                 tokens = slice(tile * P, (tile + tiles) * P)
                 bias = vec_cols[:, qk * H + head : qk * H + head + 1]
-                for table, product in ((cos_table, same), (sin_table, other)):
-                    nc.vector.scalar_tensor_tensor(
-                        out=product[:, part],
-                        in0=acc[:, part],
-                        scalar=bias,
-                        in1=table[:, qk, tokens],
-                        op0=ALU.add,
-                        op1=ALU.mult,
-                    )
+                nc.vector.scalar_tensor_tensor(
+                    out=both[:, :, part],
+                    in0=acc[:, part].unsqueeze(1).to_broadcast([P, 2, tiles * P]),
+                    scalar=bias,
+                    in1=image_table[:, qk, :, tokens],
+                    op0=ALU.add,
+                    op1=ALU.mult,
+                )
                 at += tiles * P
-            in_sbuf[u] = (squared.pop(u), same, other)
+            in_sbuf[u] = (squared.pop(u), both)
 
         def turn(u):
-            squares, same, other = in_sbuf.pop(u)
+            squares, both = in_sbuf.pop(u)
             sums = psum_sum.tile([P, 4, SUM_COLS], F32, name="sums")
             for j in range(4):
                 nc.tensor.matmul(
@@ -380,10 +379,10 @@ def tile_fluxjointattention_pa_kernel(
             )
             turned = psum_out.tile([P, 4, D], F32, name="turned")
             for j in range(4):
-                for product, matrix, first in ((same, ident, True), (other, flip, False)):
+                for which, matrix, first in ((SAME, ident, True), (OTHER, flip, False)):
                     nc.tensor.matmul(
                         out=turned[:, j, :],
-                        lhsT=product[:, j * P : (j + 1) * P],
+                        lhsT=both[:, which, j * P : (j + 1) * P],
                         rhs=matrix[:],
                         is_transpose=True,
                         start=first,
@@ -421,8 +420,15 @@ def tile_fluxjointattention_pa_kernel(
                             func=ACT.Copy,
                             scale=inv_rms[:, h * tiles + j : h * tiles + j + 1],
                         )
-            if heads == 2:
-                out_rows = token_rows(outs[qk].rearrange("b s h d -> (b s) (h d)"), 0)
+            out_rows = token_rows(outs[qk].rearrange("b s h d -> (b s) (h d)"), 0)
+            if u >= len(jobs) - 3:
+                nc.sync.dma_start(
+                    out=out_rows[:, tile : tile + tiles, head * D : (head + heads) * D],
+                    in_=result[:, tile : tile + tiles, head % 2 : head % 2 + heads, :].rearrange(
+                        "p n h d -> p n (h d)"
+                    ),
+                )
+            elif heads == 2:
                 nc.sync.dma_start(
                     out=out_rows[:, :, 2 * pair * D : 2 * (pair + 1) * D],
                     in_=result[:].rearrange("p n h d -> p n (h d)"),
@@ -530,11 +536,11 @@ def tile_fluxjointattention_pa_kernel(
         quantise_activations(TEXT_TILES + 2)
         for g in range(PASSES):
             regroup_weight(0, g, 0, SHARE_FIRST)
-        turn_tables()
         for g in range(PASSES):
             quantise_weight(0, g, 0)
+        turn_vectors()
+        turn_tables()
         build_tables(0)
-        build_tables(1)
         quantise_activations(TEXT_TILES + 4)
         for g in range(PASSES):
             regroup_weight(0, g, 1, SHARE_FIRST)
@@ -544,7 +550,7 @@ def tile_fluxjointattention_pa_kernel(
 
         IMAGE, TEXT = 0, 1
         order = [(IMAGE, u) for u in range(len(jobs))]
-        for at, text_job in ((17, (0, 0)), (20, (0, 1)), (23, (1, 0)), (26, (1, 1))):
+        for at, text_job in ((17, (0, 0)), (19, (0, 1)), (22, (1, 0)), (24, (1, 1))):
             order.insert(at, (TEXT, text_job))
 
         PROJECT, SQUARE, PRODUCTS, TURN, FINISH = range(5)
@@ -575,8 +581,10 @@ def tile_fluxjointattention_pa_kernel(
                 quantise_weight(0, s, 1)
             if s in regroup_at:
                 regroup_weight(*regroup_at[s], SHARE)
-            if s - 4 in regroup_at:
-                quantise_weight(*regroup_at[s - 4])
+            if s - 2 in regroup_at:
+                quantise_weight(*regroup_at[s - 2])
+            if s == 1:
+                build_tables(1)
             if s == 6:
                 quantise_activations(0)
             if s == 9:

@@ -31,11 +31,12 @@ TOKEN_TILES = TEXT_TILES + IMAGE_TILES
 STREAM_TILES = ((TEXT_TILES, IMAGE_TILES), (0, TEXT_TILES))
 
 HALF = HD // 2
-SHARE_FIRST = (320, 192, 0)
-SHARE = (192, 320, 0)
-GPSIMD_COLS = 64
+SHARE_FIRST = (320, 192)
+SHARE = (192, 320)
 
 SCALE_ON_VECTOR = (2, 5)
+
+GPSIMD_HEADS = 2
 
 SUM_COLS = 64
 
@@ -76,7 +77,7 @@ def tile_fluxjointattention_pa_kernel(
 
     with ExitStack() as ctx:
         keep = ctx.enter_context(tc.tile_pool(name="keep", bufs=1))
-        raw_pool = ctx.enter_context(tc.tile_pool(name="raw", bufs=2))
+        raw_pool = ctx.enter_context(tc.tile_pool(name="raw", bufs=4))
         stage = ctx.enter_context(tc.tile_pool(name="stage", bufs=3))
         work = ctx.enter_context(tc.tile_pool(name="work", bufs=3))
         psum_acc = ctx.enter_context(tc.psum_pool(name="psum_acc", bufs=4))
@@ -106,34 +107,46 @@ def tile_fluxjointattention_pa_kernel(
 
         def load_tables(stream):
             tile_lo, tiles = STREAM_TILES[stream]
-            nc.sync.dma_start(out=cos_sb[:, tile_lo : tile_lo + tiles, :], in_=token_rows(rope_cos, stream))
             nc.sync.dma_start(out=sin_sb[:, tile_lo : tile_lo + tiles, :], in_=token_rows(rope_sin, stream))
+            nc.sync.dma_start(out=cos_sb[:, tile_lo : tile_lo + tiles, :], in_=token_rows(rope_cos, stream))
 
-        def load_weight(raw, m, g, cols):
+        raws = {}
+
+        def load_weight_half(m, g, half):
+            raw_half = raw_pool.tile([P, PACK, HALF], BF16, name="raw_half", bufs=4)
+            rows = weights[m][g * K_PASS : (g + 1) * K_PASS, half * HALF : (half + 1) * HALF]
+            nc.sync.dma_start(out=raw_half[:], in_=rows.rearrange("(p t) n -> p t n", t=PACK))
+            raws[(m, g, half)] = raw_half[:]
+
+        def load_weight(m, g):
+            raw = raw_pool.tile([P, PACK, HD], BF16, name="raw", bufs=4)
+            rows = weights[m][g * K_PASS : (g + 1) * K_PASS, :]
+            nc.sync.dma_start(out=raw[:], in_=rows.rearrange("(p t) n -> p t n", t=PACK))
+            for half in range(2):
+                raws[(m, g, half)] = raw[:, :, half * HALF : (half + 1) * HALF]
+
+        def load_image(tile_lo, tiles):
             nc.sync.dma_start(
-                out=raw[:, g, :, cols],
-                in_=weights[m][g * K_PASS : (g + 1) * K_PASS, cols].rearrange("(p t) n -> p t n", t=PACK),
+                out=act_sb[:, TEXT_TILES + tile_lo : TEXT_TILES + tile_lo + tiles, :],
+                in_=image_rows[:, tile_lo : tile_lo + tiles, :],
             )
 
-        raws = []
-        for m in range(4):
-            raw = raw_pool.tile([P, PASSES, PACK, HD], BF16, name="raw")
-            raws.append(raw)
-        nc.sync.dma_start(out=act_sb[:, TEXT_TILES : TEXT_TILES + 4, :], in_=image_rows[:, :4, :])
-        for g in range(PASSES):
-            load_weight(raws[0], 0, g, slice(0, HALF))
+        load_image(0, 2)
+        load_weight_half(0, 0, 0)
+        load_image(2, 2)
         load_tables(0)
-        nc.sync.dma_start(out=act_sb[:, TEXT_TILES + 4 :, :], in_=image_rows[:, 4:, :])
+        load_weight_half(0, 1, 0)
+        load_image(4, 2)
         for g in range(PASSES):
-            load_weight(raws[0], 0, g, slice(HALF, HD))
+            load_weight_half(0, g, 1)
         for g in range(PASSES):
-            load_weight(raws[1], 1, g, slice(0, HD))
+            load_weight(1, g)
         nc.sync.dma_start(out=act_sb[:, :TEXT_TILES, :], in_=text_rows)
         load_tables(1)
         load_text_row()
         for m in (2, 3):
             for g in range(PASSES):
-                load_weight(raws[m], m, g, slice(0, HD))
+                load_weight(m, g)
 
         ident = keep.tile([P, P], F32)
         make_identity(nc, ident[:])
@@ -171,11 +184,13 @@ def tile_fluxjointattention_pa_kernel(
         image_table = keep.tile([P, 2, 2, IMAGE_TILES * P], F32)
         tables_in_psum = []
 
-        def turn_tables():
+        def swap_sines():
             swapped_pairs = sin_swapped[:].rearrange("p n (i t) -> p n t i", t=2)
             sin_pairs = sin_sb[:, TEXT_TILES:, :].rearrange("p n (i t) -> p n t i", t=2)
             for t in range(2):
-                nc.vector.tensor_copy(out=swapped_pairs[:, :, t, :], in_=sin_pairs[:, :, 1 - t, :])
+                nc.gpsimd.tensor_copy(out=swapped_pairs[:, :, t, :], in_=sin_pairs[:, :, 1 - t, :])
+
+        def turn_tables():
             for source in (cos_sb[:, TEXT_TILES:, :], sin_swapped[:]):
                 bank = psum_out.tile([P, IMAGE_TILES * P], BF16, name="turned")
                 for j in range(IMAGE_TILES):
@@ -234,7 +249,9 @@ def tile_fluxjointattention_pa_kernel(
         act_codes = keep.tile([P, PASSES, TOKEN_TILES * P], U32, align_bytes=64)
         act_scales = keep.tile([P, PASSES, TOKEN_TILES * P], U8, align_bytes=64)
 
-        def quantise_activations(first_tile):
+        turned_activations = {}
+
+        def turn_activations(first_tile):
             grouped = stage.tile([P, PASSES, 2 * P, PACK], BF16, name="act_grouped", align_bytes=64, bufs=2)
             grouped_words = grouped[:].bitcast(F32)
             for j in range(2):
@@ -252,6 +269,10 @@ def tile_fluxjointattention_pa_kernel(
                     nc.scalar.copy(out=target, in_=source)
                 else:
                     nc.vector.tensor_copy(out=target, in_=source)
+            turned_activations[first_tile] = grouped
+
+        def quantise_activations(first_tile):
+            grouped = turned_activations.pop(first_tile)
             cols = slice(first_tile * P, (first_tile + 2) * P)
             for g in range(PASSES):
                 nc.vector.quantize_mx(
@@ -266,10 +287,9 @@ def tile_fluxjointattention_pa_kernel(
         regrouped = {}
 
         def regroup_weight(m, g, half, share):
-            cols = slice(half * HALF, (half + 1) * HALF)
             grouped = stage.tile([P, HALF, PACK], BF16, name="w_grouped", align_bytes=64, bufs=4)
             dst = grouped[:].rearrange("p (c i) t -> p c t i", i=4)
-            src = raws[m][:, g, :, cols].rearrange("p t (c i) -> p c t i", i=4)
+            src = raws[(m, g, half)].rearrange("p t (c i) -> p c t i", i=4)
             lo = 0
             for engine, width in enumerate(share):
                 part = slice(lo // 4, (lo + width) // 4)
@@ -278,20 +298,8 @@ def tile_fluxjointattention_pa_kernel(
                     continue
                 if engine == 0:
                     nc.vector.tensor_copy(out=dst[:, part], in_=src[:, part])
-                elif engine == 1:
-                    nc.scalar.copy(out=dst[:, part], in_=src[:, part])
                 else:
-                    for c in range(lo - width, lo, GPSIMD_COLS):
-                        nc.gpsimd.tensor_scalar(
-                            out=grouped[:, c : c + GPSIMD_COLS, :],
-                            in0=raws[m][:, g, :, half * HALF + c : half * HALF + c + GPSIMD_COLS].rearrange(
-                                "p t c -> p c t"
-                            ),
-                            scalar1=1.0,
-                            scalar2=0.0,
-                            op0=ALU.mult,
-                            op1=ALU.add,
-                        )
+                    nc.scalar.copy(out=dst[:, part], in_=src[:, part])
             regrouped[(m, g, half)] = grouped
 
         def quantise_weight(m, g, half):
@@ -373,10 +381,6 @@ def tile_fluxjointattention_pa_kernel(
                 nc.tensor.matmul(
                     out=sums[:, j, :], lhsT=squares[:, j * P : (j + 1) * P], rhs=ones[:], start=True, stop=True
                 )
-            inv_rms = work.tile([P, 4], F32, name="inv_rms")
-            nc.scalar.activation(
-                out=inv_rms[:], in_=sums[:, :, 0], func=ACT.Abs_reciprocal_sqrt, bias=eps_col[:, 0:1], scale=1.0 / D
-            )
             turned = psum_out.tile([P, 4, D], F32, name="turned")
             for j in range(4):
                 for which, matrix, first in ((SAME, ident, True), (OTHER, flip, False)):
@@ -388,13 +392,17 @@ def tile_fluxjointattention_pa_kernel(
                         start=first,
                         stop=not first,
                     )
-            turned_back[u] = (inv_rms, turned)
+            turned_back[u] = (sums, turned)
 
         def normalise_store(u):
             qk, pair, pieces = jobs[u]
-            inv_rms, turned = turned_back.pop(u)
+            sums, turned = turned_back.pop(u)
+            inv_rms = work.tile([P, 4], F32, name="inv_rms")
+            nc.scalar.activation(
+                out=inv_rms[:], in_=sums[:, :, 0], func=ACT.Abs_reciprocal_sqrt, bias=eps_col[:, 0:1], scale=1.0 / D
+            )
             if (qk, pair) not in results:
-                result = work.tile([P, IMAGE_TILES, 2, D], F32, name="result")
+                result = work.tile([P, IMAGE_TILES, 2, D], F32, name="result", bufs=2)
                 results[(qk, pair)] = result
             result = results[(qk, pair)]
             heads = len(pieces)
@@ -468,7 +476,7 @@ def tile_fluxjointattention_pa_kernel(
         def text_products(job):
             qk, n = job
             table_ps, banks = text_state[job]
-            y = work.tile([P, H, 2, PAIRS], F32, name="y", bufs=2)
+            y = work.tile([P, H, 2, PAIRS], F32, name="y", bufs=1)
             for bank in range(HD // BANK):
                 heads = slice(bank * BANK // D, (bank + 1) * BANK // D)
                 nc.vector.tensor_tensor(
@@ -504,17 +512,22 @@ def tile_fluxjointattention_pa_kernel(
                 in1=table_ps[:, OTHER, :PAIRS].unsqueeze(1).to_broadcast([P, H, PAIRS]),
                 op=ALU.mult,
             )
-            nc.gpsimd.tensor_tensor(
-                out=text_other[:, :, 1, :],
-                in0=y[:, :, 0, :],
-                in1=text_table[:, n, qk, OTHER, PAIRS:].unsqueeze(1).to_broadcast([P, H, PAIRS]),
-                op=ALU.mult,
-            )
+            for h in range(0, H, GPSIMD_HEADS):
+                nc.gpsimd.tensor_tensor(
+                    out=text_other[:, h : h + GPSIMD_HEADS, 1, :],
+                    in0=y[:, h : h + GPSIMD_HEADS, 0, :],
+                    in1=text_table[:, n, qk, OTHER, PAIRS:].unsqueeze(1).to_broadcast([P, GPSIMD_HEADS, PAIRS]),
+                    op=ALU.mult,
+                )
             text_state[job] = (text_same, text_other, text_inv)
 
         def text_add(job):
             text_same, text_other, text_inv = text_state[job]
-            nc.gpsimd.tensor_tensor(out=text_same[:], in0=text_same[:], in1=text_other[:], op=ALU.add)
+            for h in range(0, H, GPSIMD_HEADS):
+                heads = slice(h, h + GPSIMD_HEADS)
+                nc.gpsimd.tensor_tensor(
+                    out=text_same[:, heads], in0=text_same[:, heads], in1=text_other[:, heads], op=ALU.add
+                )
 
         def text_finish(job):
             qk, n = job
@@ -532,15 +545,20 @@ def tile_fluxjointattention_pa_kernel(
                 out=out_rows[:, n, :], in_=text_result[:].rearrange("p h i t -> p (h i t)")
             )
 
-        quantise_activations(TEXT_TILES)
-        quantise_activations(TEXT_TILES + 2)
-        for g in range(PASSES):
-            regroup_weight(0, g, 0, SHARE_FIRST)
-        for g in range(PASSES):
-            quantise_weight(0, g, 0)
-        turn_vectors()
-        turn_tables()
-        build_tables(0)
+        with tc.manual_schedule():
+            turn_activations(TEXT_TILES)
+            swap_sines()
+            regroup_weight(0, 0, 0, SHARE_FIRST)
+            quantise_activations(TEXT_TILES)
+            turn_activations(TEXT_TILES + 2)
+            turn_vectors()
+            turn_tables()
+            regroup_weight(0, 1, 0, SHARE_FIRST)
+            quantise_weight(0, 0, 0)
+            quantise_activations(TEXT_TILES + 2)
+            quantise_weight(0, 1, 0)
+            build_tables(0)
+        turn_activations(TEXT_TILES + 4)
         quantise_activations(TEXT_TILES + 4)
         for g in range(PASSES):
             regroup_weight(0, g, 1, SHARE_FIRST)
@@ -586,6 +604,7 @@ def tile_fluxjointattention_pa_kernel(
             if s == 1:
                 build_tables(1)
             if s == 6:
+                turn_activations(0)
                 quantise_activations(0)
             if s == 9:
                 spread_text_gains()

@@ -32,7 +32,7 @@ STREAM_TILES = ((TEXT_TILES, IMAGE_TILES), (0, TEXT_TILES))
 
 HALF = HD // 2
 SHARE_FIRST = (320, 192)
-SHARE = (192, 320)
+SHARE = (224, 288)
 
 SCALE_ON_VECTOR = (2, 5)
 
@@ -89,15 +89,14 @@ def tile_fluxjointattention_pa_kernel(
         for m in range(2):
             nc.scalar.dma_start(out=vec_rows[m * H : (m + 1) * H, :], in_=biases[m].rearrange("(h d) -> h d", h=H))
             nc.scalar.dma_start(out=vec_rows[2 * H + m : 2 * H + m + 1, :], in_=gains[m].unsqueeze(0))
-        text_row = keep.tile([P, 2 * D + 2 * HD], BF16)
+        text_gain = keep.tile([P, 2, D], BF16)
+        text_row = keep.tile([P, 2 * HD], BF16)
         nc.vector.memset(text_row[:].bitcast(I32), 0)
 
-        def load_text_row():
+        def load_text_vectors():
             for qk in range(2):
-                nc.sync.dma_start(out=text_row[0:1, qk * D : (qk + 1) * D], in_=gains[2 + qk].unsqueeze(0))
-                nc.sync.dma_start(
-                    out=text_row[0:1, 2 * D + qk * HD : 2 * D + (qk + 1) * HD], in_=biases[2 + qk].unsqueeze(0)
-                )
+                nc.sync.dma_start(out=text_gain[:, qk, :], in_=gains[2 + qk].partition_broadcast(P))
+                nc.sync.dma_start(out=text_row[0:1, qk * HD : (qk + 1) * HD], in_=biases[2 + qk].unsqueeze(0))
 
         act_sb = keep.tile([P, TOKEN_TILES, DM], BF16)
         cos_sb = keep.tile([P, TOKEN_TILES, D], BF16)
@@ -143,7 +142,7 @@ def tile_fluxjointattention_pa_kernel(
             load_weight(1, g)
         nc.sync.dma_start(out=act_sb[:, :TEXT_TILES, :], in_=text_rows)
         load_tables(1)
-        load_text_row()
+        load_text_vectors()
         for m in (2, 3):
             for g in range(PASSES):
                 load_weight(m, g)
@@ -214,36 +213,35 @@ def tile_fluxjointattention_pa_kernel(
             return bank
 
         text_bias = keep.tile([P, 2, H, 2, PAIRS], BF16)
-        gain_same = keep.tile([P, 2, 2, PAIRS], F32)
-        gain_other = keep.tile([P, 2, 2, PAIRS], F32)
+        odd_gain_negated = keep.tile([P, 2, PAIRS], BF16)
         text_table = keep.tile([P, TEXT_TILES, 2, 2, D], F32)
-
-        def spread_text_gains():
-            pairs = spread(0, 2 * D)[:].rearrange("p (s i t) -> p s i t", s=2, t=2)
-            nc.vector.tensor_copy(out=gain_same[:], in_=pairs.rearrange("p s i t -> p s t i"))
-            nc.vector.tensor_scalar_mul(out=gain_other[:, :, 0, :], in0=pairs[:, :, :, 1], scalar1=-1.0)
-            nc.vector.tensor_copy(out=gain_other[:, :, 1, :], in_=pairs[:, :, :, 0])
 
         def spread_text_bias(qk):
             for bank in range(HD // BANK):
                 heads = slice(bank * BANK // D, (bank + 1) * BANK // D)
                 nc.scalar.copy(
                     out=text_bias[:, qk, heads, :, :],
-                    in_=spread(2 * D + qk * HD + bank * BANK, BANK)[:].rearrange(
+                    in_=spread(qk * HD + bank * BANK, BANK)[:].rearrange(
                         "p (h i t) -> p h t i", t=2, h=BANK // D
                     ),
                 )
 
         def build_text_tables():
-            shape = [P, TEXT_TILES, 2, PAIRS]
+            gain_pairs = text_gain[:].rearrange("p s (i t) -> p s t i", t=2)
+            nc.gpsimd.tensor_scalar_mul(out=odd_gain_negated[:], in0=gain_pairs[:, :, 1, :], scalar1=-1.0)
+            cos_pairs = cos_sb[:, :TEXT_TILES, :].rearrange("p n (i t) -> p n t i", t=2)
+            sin_pairs = sin_sb[:, :TEXT_TILES, :].rearrange("p n (i t) -> p n t i", t=2)
             for qk in range(2):
-                for which, source, gain in ((SAME, cos_sb, gain_same), (OTHER, sin_sb, gain_other)):
-                    nc.vector.tensor_tensor(
-                        out=text_table[:, :, qk, which, :].rearrange("p n (t i) -> p n t i", t=2),
-                        in0=source[:, :TEXT_TILES, :].rearrange("p n (i t) -> p n t i", t=2),
-                        in1=gain[:, qk, :, :].unsqueeze(1).to_broadcast(shape),
-                        op=ALU.mult,
-                    )
+                same_gains = (gain_pairs[:, qk, 0, :], gain_pairs[:, qk, 1, :])
+                other_gains = (odd_gain_negated[:, qk, :], gain_pairs[:, qk, 0, :])
+                for which, source, gains_of in ((SAME, cos_pairs, same_gains), (OTHER, sin_pairs, other_gains)):
+                    for t in range(2):
+                        nc.gpsimd.tensor_tensor(
+                            out=text_table[:, :, qk, which, t * PAIRS : (t + 1) * PAIRS],
+                            in0=source[:, :, t, :],
+                            in1=gains_of[t].unsqueeze(1).to_broadcast([P, TEXT_TILES, PAIRS]),
+                            op=ALU.mult,
+                        )
 
         act_words = act_sb[:].bitcast(F32)
         act_codes = keep.tile([P, PASSES, TOKEN_TILES * P], U32, align_bytes=64)
@@ -607,7 +605,6 @@ def tile_fluxjointattention_pa_kernel(
                 turn_activations(0)
                 quantise_activations(0)
             if s == 9:
-                spread_text_gains()
                 spread_text_bias(0)
                 spread_text_bias(1)
                 build_text_tables()

from contextlib import ExitStack

import concourse.mybir as mybir
from concourse.masks import make_identity

F32 = mybir.dt.float32
BF16 = mybir.dt.bfloat16
U32 = mybir.dt.uint32
U8 = mybir.dt.uint8
I32 = mybir.dt.int32
FP8X4 = mybir.dt.float8_e4m3fn_x4
ALU = mybir.AluOpType
ACT = mybir.ActivationFunctionType
AXIS = mybir.AxisListType

P = 128
PACK = 4
K_PASS = P * PACK
DM = 1024
PASSES = DM // K_PASS
H = 8
D = 128
HD = H * D
PAIRS = D // 2
BANK = 512
EPS = 1e-6

TEXT_TILES = 2
IMAGE_TILES = 6
TOKEN_TILES = TEXT_TILES + IMAGE_TILES
STREAM_TILES = ((TEXT_TILES, IMAGE_TILES), (0, TEXT_TILES))

HALF = HD // 2
SHARE_FIRST = (320, 192)
SHARE = (224, 288)

SCALE_ON_VECTOR = (2, 5)

GPSIMD_HEADS = 2

SUM_COLS = 64

FLOPS = 2 * (TOKEN_TILES * P) * DM * (2 * HD)


def tile_fluxjointattention_pa_kernel(
    tc,
    hidden_states,
    encoder_hidden_states,
    rope_cos,
    rope_sin,
    Wq,
    Wk,
    Waq,
    Wak,
    bq,
    bk,
    baq,
    bak,
    g_q,
    g_k,
    g_aq,
    g_ak,
    out_0,
    out_1,
):
    nc = tc.nc
    weights = (Wq, Wk, Waq, Wak)
    biases = (bq, bk, baq, bak)
    gains = (g_q, g_k, g_aq, g_ak)
    outs = (out_0, out_1)

    def token_rows(dram_rows, stream):
        tile_lo, tiles = STREAM_TILES[stream]
        rows = dram_rows[tile_lo * P : (tile_lo + tiles) * P, :]
        return rows.rearrange("(p n) c -> p n c", n=tiles)

    with ExitStack() as ctx:
        keep = ctx.enter_context(tc.tile_pool(name="keep", bufs=1))
        raw_pool = ctx.enter_context(tc.tile_pool(name="raw", bufs=4))
        stage = ctx.enter_context(tc.tile_pool(name="stage", bufs=3))
        work = ctx.enter_context(tc.tile_pool(name="work", bufs=3))
        psum_acc = ctx.enter_context(tc.psum_pool(name="psum_acc", bufs=4))
        psum_out = ctx.enter_context(tc.psum_pool(name="psum_out", bufs=2))
        psum_sum = ctx.enter_context(tc.psum_pool(name="psum_sum", bufs=2))

        vec_rows = keep.tile([P, P], BF16)
        nc.gpsimd.memset(vec_rows[:].bitcast(I32), 0)
        for m in range(2):
            nc.scalar.dma_start(out=vec_rows[m * H : (m + 1) * H, :], in_=biases[m].rearrange("(h d) -> h d", h=H))
            nc.scalar.dma_start(out=vec_rows[2 * H + m : 2 * H + m + 1, :], in_=gains[m].unsqueeze(0))
        text_gain = keep.tile([P, 2, D], BF16)
        text_row = keep.tile([P, 2 * HD], BF16)
        nc.vector.memset(text_row[:].bitcast(I32), 0)

        def load_text_vectors():
            for qk in range(2):
                nc.sync.dma_start(out=text_gain[:, qk, :], in_=gains[2 + qk].partition_broadcast(P))
                nc.sync.dma_start(out=text_row[0:1, qk * HD : (qk + 1) * HD], in_=biases[2 + qk].unsqueeze(0))

        act_sb = keep.tile([P, TOKEN_TILES, DM], BF16)
        cos_sb = keep.tile([P, TOKEN_TILES, D], BF16)
        sin_sb = keep.tile([P, TOKEN_TILES, D], BF16)
        image_rows = hidden_states.rearrange("b (p n) k -> p (b n) k", n=IMAGE_TILES)
        text_rows = encoder_hidden_states.rearrange("b (p n) k -> p (b n) k", n=TEXT_TILES)

        def load_tables(stream):
            tile_lo, tiles = STREAM_TILES[stream]
            nc.sync.dma_start(out=sin_sb[:, tile_lo : tile_lo + tiles, :], in_=token_rows(rope_sin, stream))
            nc.sync.dma_start(out=cos_sb[:, tile_lo : tile_lo + tiles, :], in_=token_rows(rope_cos, stream))

        raws = {}

        def load_weight_half(m, g, half):
            raw_half = raw_pool.tile([P, PACK, HALF], BF16, name="raw_half", bufs=4)
            rows = weights[m][g * K_PASS : (g + 1) * K_PASS, half * HALF : (half + 1) * HALF]
            nc.sync.dma_start(out=raw_half[:], in_=rows.rearrange("(p t) n -> p t n", t=PACK))
            raws[(m, g, half)] = raw_half[:]

        def load_weight(m, g):
            raw = raw_pool.tile([P, PACK, HD], BF16, name="raw", bufs=4)
            rows = weights[m][g * K_PASS : (g + 1) * K_PASS, :]
            nc.sync.dma_start(out=raw[:], in_=rows.rearrange("(p t) n -> p t n", t=PACK))
            for half in range(2):
                raws[(m, g, half)] = raw[:, :, half * HALF : (half + 1) * HALF]

        def load_image(tile_lo, tiles):
            nc.sync.dma_start(
                out=act_sb[:, TEXT_TILES + tile_lo : TEXT_TILES + tile_lo + tiles, :],
                in_=image_rows[:, tile_lo : tile_lo + tiles, :],
            )

        load_image(0, 2)
        load_weight_half(0, 0, 0)
        load_image(2, 2)
        load_tables(0)
        load_weight_half(0, 1, 0)
        load_image(4, 2)
        for g in range(PASSES):
            load_weight_half(0, g, 1)
        for g in range(PASSES):
            load_weight(1, g)
        nc.sync.dma_start(out=act_sb[:, :TEXT_TILES, :], in_=text_rows)
        load_tables(1)
        load_text_vectors()
        for m in (2, 3):
            for g in range(PASSES):
                load_weight(m, g)

        ident = keep.tile([P, P], F32)
        make_identity(nc, ident[:])
        ident_bf = keep.tile([P, P], BF16)
        nc.vector.tensor_copy(out=ident_bf[:], in_=ident[:])
        flip = keep.tile([P, P], F32)
        ident_pairs = ident[:].rearrange("p (i t) -> p t i", t=2)
        flip_pairs = flip[:].rearrange("p (i t) -> p t i", t=2)
        for t in range(2):
            nc.vector.tensor_copy(out=flip_pairs[:, t, :], in_=ident_pairs[:, 1 - t, :])
        parity = keep.tile([P, 2], F32)
        nc.vector.tensor_reduce(out=parity[:], in_=ident_pairs, axis=AXIS.X, op=ALU.add)
        sign = keep.tile([P, 1], F32)
        nc.vector.tensor_sub(out=sign[:], in0=parity[:, 0:1], in1=parity[:, 1:2])
        eps_col = keep.tile([P, 1], F32)
        nc.vector.memset(eps_col[:], EPS)
        ones = keep.tile([P, SUM_COLS], F32)
        nc.vector.memset(ones[:], 1.0)
        ones_bf = keep.tile([P, P], BF16)
        nc.vector.memset(ones_bf[:], 1.0)
        warm = keep.tile([P, 1], F32)
        nc.scalar.activation(out=warm[:], in_=eps_col[:], func=ACT.Abs_reciprocal_sqrt)

        vec_cols = keep.tile([P, 2 * H + 2], F32)
        signed_gain = keep.tile([P, 2], F32)

        def turn_vectors():
            vec_ps = psum_sum.tile([P, P], BF16, name="sums")
            nc.tensor.transpose(out=vec_ps[:], in_=vec_rows[:], identity=ident_bf[:])
            nc.vector.tensor_copy(out=vec_cols[:], in_=vec_ps[:, : 2 * H + 2])
            nc.vector.tensor_scalar_mul(out=signed_gain[:], in0=vec_cols[:, 2 * H :], scalar1=sign[:, 0:1])

        SAME, OTHER = 0, 1
        sin_swapped = keep.tile([P, IMAGE_TILES, D], BF16)
        image_table = keep.tile([P, 2, 2, IMAGE_TILES * P], F32)
        tables_in_psum = []

        def swap_sines():
            swapped_pairs = sin_swapped[:].rearrange("p n (i t) -> p n t i", t=2)
            sin_pairs = sin_sb[:, TEXT_TILES:, :].rearrange("p n (i t) -> p n t i", t=2)
            for t in range(2):
                nc.gpsimd.tensor_copy(out=swapped_pairs[:, :, t, :], in_=sin_pairs[:, :, 1 - t, :])

        def turn_tables():
            for source in (cos_sb[:, TEXT_TILES:, :], sin_swapped[:]):
                bank = psum_out.tile([P, IMAGE_TILES * P], BF16, name="turned")
                for j in range(IMAGE_TILES):
                    nc.tensor.transpose(
                        out=bank[:, j * P : (j + 1) * P], in_=source[:, j, :], identity=ident_bf[:]
                    )
                tables_in_psum.append(bank)

        def build_tables(qk):
            cos_ps, sin_ps = tables_in_psum
            nc.scalar.activation(
                out=image_table[:, qk, SAME, :], in_=cos_ps[:], func=ACT.Copy, scale=vec_cols[:, 2 * H + qk : 2 * H + qk + 1]
            )
            nc.vector.tensor_scalar_mul(out=image_table[:, qk, OTHER, :], in0=sin_ps[:], scalar1=signed_gain[:, qk : qk + 1])

        def spread(col_lo, width):
            bank = psum_sum.tile([P, width], F32, name="sums")
            nc.tensor.matmul(
                out=bank[:], lhsT=ones_bf[:], rhs=text_row[:, col_lo : col_lo + width], start=True, stop=True
            )
            return bank

        text_bias = keep.tile([P, 2, H, 2, PAIRS], BF16)
        odd_gain_negated = keep.tile([P, 2, PAIRS], BF16)
        text_table = keep.tile([P, TEXT_TILES, 2, 2, D], F32)

        def spread_text_bias(qk):
            for bank in range(HD // BANK):
                heads = slice(bank * BANK // D, (bank + 1) * BANK // D)
                nc.scalar.copy(
                    out=text_bias[:, qk, heads, :, :],
                    in_=spread(qk * HD + bank * BANK, BANK)[:].rearrange(
                        "p (h i t) -> p h t i", t=2, h=BANK // D
                    ),
                )

        def build_text_tables():
            gain_pairs = text_gain[:].rearrange("p s (i t) -> p s t i", t=2)
            nc.gpsimd.tensor_scalar_mul(out=odd_gain_negated[:], in0=gain_pairs[:, :, 1, :], scalar1=-1.0)
            cos_pairs = cos_sb[:, :TEXT_TILES, :].rearrange("p n (i t) -> p n t i", t=2)
            sin_pairs = sin_sb[:, :TEXT_TILES, :].rearrange("p n (i t) -> p n t i", t=2)
            for qk in range(2):
                same_gains = (gain_pairs[:, qk, 0, :], gain_pairs[:, qk, 1, :])
                other_gains = (odd_gain_negated[:, qk, :], gain_pairs[:, qk, 0, :])
                for which, source, gains_of in ((SAME, cos_pairs, same_gains), (OTHER, sin_pairs, other_gains)):
                    for t in range(2):
                        nc.gpsimd.tensor_tensor(
                            out=text_table[:, :, qk, which, t * PAIRS : (t + 1) * PAIRS],
                            in0=source[:, :, t, :],
                            in1=gains_of[t].unsqueeze(1).to_broadcast([P, TEXT_TILES, PAIRS]),
                            op=ALU.mult,
                        )

        act_words = act_sb[:].bitcast(F32)
        act_codes = keep.tile([P, PASSES, TOKEN_TILES * P], U32, align_bytes=64)
        act_scales = keep.tile([P, PASSES, TOKEN_TILES * P], U8, align_bytes=64)

        turned_activations = {}

        def turn_activations(first_tile):
            grouped = stage.tile([P, PASSES, 2 * P, PACK], BF16, name="act_grouped", align_bytes=64, bufs=2)
            grouped_words = grouped[:].bitcast(F32)
            for j in range(2):
                turned = psum_acc.tile([P, PASSES, 2, P], F32, name="acc")
                for g in range(PASSES):
                    for u in range(2):
                        nc.tensor.transpose(
                            out=turned[:, g, u, :],
                            in_=act_words[:, first_tile + j, 2 * P * g + u : 2 * P * (g + 1) : 2],
                            identity=ident[:],
                        )
                target = grouped_words[:, :, j * P : (j + 1) * P, :]
                source = turned[:].rearrange("p g u r -> p g r u")
                if j == 0:
                    nc.scalar.copy(out=target, in_=source)
                else:
                    nc.vector.tensor_copy(out=target, in_=source)
            turned_activations[first_tile] = grouped

        def quantise_activations(first_tile):
            grouped = turned_activations.pop(first_tile)
            cols = slice(first_tile * P, (first_tile + 2) * P)
            for g in range(PASSES):
                nc.vector.quantize_mx(
                    out=act_codes[:, g, cols].bitcast(FP8X4),
                    scales=act_scales[:, g, cols],
                    in_=grouped[:, g, :, :].rearrange("p r j -> p (r j)"),
                )

        w_codes = keep.tile([P, 4, PASSES, HD], U32, align_bytes=64)
        w_scales = keep.tile([P, 4, PASSES, HD], U8, align_bytes=64)

        regrouped = {}

        def regroup_weight(m, g, half, share):
            grouped = stage.tile([P, HALF, PACK], BF16, name="w_grouped", align_bytes=64, bufs=4)
            dst = grouped[:].rearrange("p (c i) t -> p c t i", i=4)
            src = raws[(m, g, half)].rearrange("p t (c i) -> p c t i", i=4)
            lo = 0
            for engine, width in enumerate(share):
                part = slice(lo // 4, (lo + width) // 4)
                lo += width
                if width == 0:
                    continue
                if engine == 0:
                    nc.vector.tensor_copy(out=dst[:, part], in_=src[:, part])
                else:
                    nc.scalar.copy(out=dst[:, part], in_=src[:, part])
            regrouped[(m, g, half)] = grouped

        def quantise_weight(m, g, half):
            cols = slice(half * HALF, (half + 1) * HALF)
            nc.vector.quantize_mx(
                out=w_codes[:, m, g, cols].bitcast(FP8X4),
                scales=w_scales[:, m, g, cols],
                in_=regrouped.pop((m, g, half))[:].rearrange("p c t -> p (c t)"),
            )

        jobs = []
        for qk in range(2):
            for pair in range(H // 2):
                a, b = 2 * pair, 2 * pair + 1
                jobs.append((qk, pair, ((a, 0, 4),)))
                jobs.append((qk, pair, ((b, 0, 4),)))
                jobs.append((qk, pair, ((a, 4, 2), (b, 4, 2))))
        in_psum, squared, in_sbuf, turned_back, results = {}, {}, {}, {}, {}

        def project(u):
            qk, pair, pieces = jobs[u]
            acc = psum_acc.tile([P, BANK], F32, name="acc")
            at = 0
            for head, tile, tiles in pieces:
                tokens = slice((TEXT_TILES + tile) * P, (TEXT_TILES + tile + tiles) * P)
                cols = slice(head * D, (head + 1) * D)
                for g in range(PASSES):
                    nc.tensor.matmul_mx(
                        out=acc[:, at : at + tiles * P],
                        lhsT=w_codes[:, qk, g, cols].bitcast(FP8X4),
                        lhsT_scale=w_scales[:, qk, g, cols],
                        rhs=act_codes[:, g, tokens].bitcast(FP8X4),
                        rhs_scale=act_scales[:, g, tokens],
                        start=(g == 0),
                        stop=(g == PASSES - 1),
                    )
                at += tiles * P
            in_psum[u] = acc

        def square(u):
            qk, pair, pieces = jobs[u]
            squares = work.tile([P, BANK], F32, name="squares")
            at = 0
            for head, tile, tiles in pieces:
                part = slice(at, at + tiles * P)
                nc.scalar.activation(
                    out=squares[:, part],
                    in_=in_psum[u][:, part],
                    func=ACT.Square,
                    bias=vec_cols[:, qk * H + head : qk * H + head + 1],
                )
                at += tiles * P
            squared[u] = squares

        def products(u):
            qk, pair, pieces = jobs[u]
            acc = in_psum.pop(u)
            both = work.tile([P, 2, BANK], F32, name="both")
            at = 0
            for head, tile, tiles in pieces:
                part = slice(at, at + tiles * P)
                tokens = slice(tile * P, (tile + tiles) * P)
                bias = vec_cols[:, qk * H + head : qk * H + head + 1]
                nc.vector.scalar_tensor_tensor(
                    out=both[:, :, part],
                    in0=acc[:, part].unsqueeze(1).to_broadcast([P, 2, tiles * P]),
                    scalar=bias,
                    in1=image_table[:, qk, :, tokens],
                    op0=ALU.add,
                    op1=ALU.mult,
                )
                at += tiles * P
            in_sbuf[u] = (squared.pop(u), both)

        def turn(u):
            squares, both = in_sbuf.pop(u)
            sums = psum_sum.tile([P, 4, SUM_COLS], F32, name="sums")
            for j in range(4):
                nc.tensor.matmul(
                    out=sums[:, j, :], lhsT=squares[:, j * P : (j + 1) * P], rhs=ones[:], start=True, stop=True
                )
            turned = psum_out.tile([P, 4, D], F32, name="turned")
            for j in range(4):
                for which, matrix, first in ((SAME, ident, True), (OTHER, flip, False)):
                    nc.tensor.matmul(
                        out=turned[:, j, :],
                        lhsT=both[:, which, j * P : (j + 1) * P],
                        rhs=matrix[:],
                        is_transpose=True,
                        start=first,
                        stop=not first,
                    )
            turned_back[u] = (sums, turned)

        def normalise_store(u):
            qk, pair, pieces = jobs[u]
            sums, turned = turned_back.pop(u)
            inv_rms = work.tile([P, 4], F32, name="inv_rms")
            nc.scalar.activation(
                out=inv_rms[:], in_=sums[:, :, 0], func=ACT.Abs_reciprocal_sqrt, bias=eps_col[:, 0:1], scale=1.0 / D
            )
            if (qk, pair) not in results:
                result = work.tile([P, IMAGE_TILES, 2, D], F32, name="result", bufs=2)
                results[(qk, pair)] = result
            result = results[(qk, pair)]
            heads = len(pieces)
            head, tile, tiles = pieces[0]
            target = result[:, tile : tile + tiles, head % 2 : head % 2 + heads, :].rearrange("p j h d -> p h j d")
            source = turned[:].rearrange("p (h j) d -> p h j d", h=heads)
            if u % 8 in SCALE_ON_VECTOR:
                nc.vector.tensor_tensor(
                    out=target,
                    in0=source,
                    in1=inv_rms[:]
                    .rearrange("p (h j) -> p h j", h=heads)
                    .unsqueeze(3)
                    .to_broadcast([P, heads, tiles, D]),
                    op=ALU.mult,
                )
            else:
                for h in range(heads):
                    for j in range(tiles):
                        nc.scalar.activation(
                            out=target[:, h, j, :],
                            in_=source[:, h, j, :],
                            func=ACT.Copy,
                            scale=inv_rms[:, h * tiles + j : h * tiles + j + 1],
                        )
            out_rows = token_rows(outs[qk].rearrange("b s h d -> (b s) (h d)"), 0)
            if u >= len(jobs) - 3:
                nc.sync.dma_start(
                    out=out_rows[:, tile : tile + tiles, head * D : (head + heads) * D],
                    in_=result[:, tile : tile + tiles, head % 2 : head % 2 + heads, :].rearrange(
                        "p n h d -> p n (h d)"
                    ),
                )
            elif heads == 2:
                nc.sync.dma_start(
                    out=out_rows[:, :, 2 * pair * D : 2 * (pair + 1) * D],
                    in_=result[:].rearrange("p n h d -> p n (h d)"),
                )

        text_state = {}

        def text_project(job):
            qk, n = job
            m = 2 + qk
            table_ps = psum_sum.tile([P, 2, D], F32, name="sums")
            nc.tensor.matmul(
                out=table_ps[:].rearrange("p s d -> p (s d)"),
                lhsT=ident[:],
                rhs=text_table[:, n, qk, :, :].rearrange("p s d -> p (s d)"),
                start=True,
                stop=True,
            )
            tokens = slice(n * P, (n + 1) * P)
            banks = []
            for bank in range(HD // BANK):
                cols = slice(bank * BANK, (bank + 1) * BANK)
                acc = psum_acc.tile([P, BANK], F32, name="acc")
                for g in range(PASSES):
                    nc.tensor.matmul_mx(
                        out=acc[:],
                        lhsT=act_codes[:, g, tokens].bitcast(FP8X4),
                        lhsT_scale=act_scales[:, g, tokens],
                        rhs=w_codes[:, m, g, cols].bitcast(FP8X4),
                        rhs_scale=w_scales[:, m, g, cols],
                        start=(g == 0),
                        stop=(g == PASSES - 1),
                    )
                banks.append(acc)
            text_state[job] = (table_ps, banks)

        def text_products(job):
            qk, n = job
            table_ps, banks = text_state[job]
            y = work.tile([P, H, 2, PAIRS], F32, name="y", bufs=1)
            for bank in range(HD // BANK):
                heads = slice(bank * BANK // D, (bank + 1) * BANK // D)
                nc.vector.tensor_tensor(
                    out=y[:, heads, :, :],
                    in0=banks[bank][:].rearrange("p (h i t) -> p h t i", t=2, h=BANK // D),
                    in1=text_bias[:, qk, heads, :, :],
                    op=ALU.add,
                )
            sumsq = work.tile([P, H], F32, name="sumsq")
            for h in range(H):
                text_squares = work.tile([P, D], BF16, name="text_squares")
                nc.scalar.activation(
                    out=text_squares[:],
                    in_=y[:, h, :, :].rearrange("p t i -> p (t i)"),
                    func=ACT.Square,
                    accum_out=sumsq[:, h : h + 1],
                )
            text_inv = work.tile([P, H], F32, name="text_inv")
            nc.scalar.activation(
                out=text_inv[:], in_=sumsq[:], func=ACT.Abs_reciprocal_sqrt, bias=eps_col[:, 0:1], scale=1.0 / D
            )
            text_same = work.tile([P, H, 2, PAIRS], F32, name="text_same", bufs=2)
            nc.vector.tensor_tensor(
                out=text_same[:].rearrange("p h t i -> p h (t i)"),
                in0=y[:].rearrange("p h t i -> p h (t i)"),
                in1=table_ps[:, SAME, :].unsqueeze(1).to_broadcast([P, H, D]),
                op=ALU.mult,
            )
            text_other = work.tile([P, H, 2, PAIRS], F32, name="text_other", bufs=2)
            nc.vector.tensor_tensor(
                out=text_other[:, :, 0, :],
                in0=y[:, :, 1, :],
                in1=table_ps[:, OTHER, :PAIRS].unsqueeze(1).to_broadcast([P, H, PAIRS]),
                op=ALU.mult,
            )
            for h in range(0, H, GPSIMD_HEADS):
                nc.gpsimd.tensor_tensor(
                    out=text_other[:, h : h + GPSIMD_HEADS, 1, :],
                    in0=y[:, h : h + GPSIMD_HEADS, 0, :],
                    in1=text_table[:, n, qk, OTHER, PAIRS:].unsqueeze(1).to_broadcast([P, GPSIMD_HEADS, PAIRS]),
                    op=ALU.mult,
                )
            text_state[job] = (text_same, text_other, text_inv)

        def text_add(job):
            text_same, text_other, text_inv = text_state[job]
            for h in range(0, H, GPSIMD_HEADS):
                heads = slice(h, h + GPSIMD_HEADS)
                nc.gpsimd.tensor_tensor(
                    out=text_same[:, heads], in0=text_same[:, heads], in1=text_other[:, heads], op=ALU.add
                )

        def text_finish(job):
            qk, n = job
            text_same, text_other, text_inv = text_state.pop(job)
            text_result = work.tile([P, H, PAIRS, 2], F32, name="text_result", bufs=2)
            for h in range(H):
                nc.scalar.activation(
                    out=text_result[:, h, :, :],
                    in_=text_same[:, h, :, :].rearrange("p t i -> p i t"),
                    func=ACT.Copy,
                    scale=text_inv[:, h : h + 1],
                )
            out_rows = token_rows(outs[qk].rearrange("b s h d -> (b s) (h d)"), 1)
            nc.sync.dma_start(
                out=out_rows[:, n, :], in_=text_result[:].rearrange("p h i t -> p (h i t)")
            )

        with tc.manual_schedule():
            turn_activations(TEXT_TILES)
            swap_sines()
            regroup_weight(0, 0, 0, SHARE_FIRST)
            quantise_activations(TEXT_TILES)
            turn_activations(TEXT_TILES + 2)
            turn_vectors()
            turn_tables()
            regroup_weight(0, 1, 0, SHARE_FIRST)
            quantise_weight(0, 0, 0)
            quantise_activations(TEXT_TILES + 2)
            quantise_weight(0, 1, 0)
            build_tables(0)
        turn_activations(TEXT_TILES + 4)
        quantise_activations(TEXT_TILES + 4)
        for g in range(PASSES):
            regroup_weight(0, g, 1, SHARE_FIRST)

        pieces_due = [(m, g, half) for m in (1, 2, 3) for half in range(2) for g in range(PASSES)]
        regroup_at = {i * 3 // 2: piece for i, piece in enumerate(pieces_due)}

        IMAGE, TEXT = 0, 1
        order = [(IMAGE, u) for u in range(len(jobs))]
        for at, text_job in ((17, (0, 0)), (19, (0, 1)), (22, (1, 0)), (24, (1, 1))):
            order.insert(at, (TEXT, text_job))

        PROJECT, SQUARE, PRODUCTS, TURN, FINISH = range(5)
        stages = (
            (project, text_project),
            (square, None),
            (products, text_products),
            (turn, text_add),
            (normalise_store, text_finish),
        )

        def run(stage, at):
            if 0 <= at < len(order):
                kind, job = order[at]
                if stages[stage][kind] is not None:
                    stages[stage][kind](job)

        run(PROJECT, 0)
        run(PROJECT, 1)
        run(SQUARE, 0)
        for s in range(len(order) + 2):
            run(TURN, s - 1)
            run(PROJECT, s + 2)
            run(SQUARE, s + 1)
            run(PRODUCTS, s)
            run(FINISH, s - 2)
            if s < PASSES:
                quantise_weight(0, s, 1)
            if s in regroup_at:
                regroup_weight(*regroup_at[s], SHARE)
            if s - 2 in regroup_at:
                quantise_weight(*regroup_at[s - 2])
            if s == 1:
                build_tables(1)
            if s == 6:
                turn_activations(0)
                quantise_activations(0)
            if s == 9:
                spread_text_bias(0)
                spread_text_bias(1)
                build_text_tables()
